import numpy as np
import ml_dtypes


def mxq(x, axis, fmt="e4m3"):
    dtype, down = {"e4m3": (ml_dtypes.float8_e4m3fn, 7), "e5m2": (ml_dtypes.float8_e5m2, 14)}[fmt]
    v = np.moveaxis(np.asarray(x, np.float32).astype(ml_dtypes.bfloat16).astype(np.float64), axis, -1)
    blocks = v.reshape(v.shape[:-1] + (-1, 32))
    amax = np.abs(blocks).max(-1, keepdims=True)
    byte = np.maximum(np.where(amax > 0, np.frexp(amax)[1] - 1 + 127, 0) - down, 1)
    scale = np.exp2(byte - 127.0)
    codes = (blocks / scale).astype(np.float32).astype(dtype).astype(np.float64)
    return np.moveaxis((codes * scale).reshape(v.shape), -1, axis)


WIDE = False


def mx_kscale(k):
    if not WIDE:
        return np.ones(k)
    levels = np.array([10, -10, 5, -5, 0])
    a = np.random.permutation(np.resize(levels, k // 512 * 4)).reshape(k // 512, 4)
    idx = np.arange(k)
    return np.exp2(a[idx // 512, idx % 128 // 32])


BF16 = ml_dtypes.bfloat16


def bf(x):
    return np.asarray(x, np.float32).astype(BF16)


def f64(x):
    return np.asarray(x).astype(np.float64)


E2M1 = np.array([0.0, 0.5, 1.0, 1.5, 2.0, 3.0, 4.0, 6.0, -0.0, -0.5, -1.0, -1.5, -2.0, -3.0, -4.0, -6.0])


def pack_weight(w, fmt):
    k, n = w.shape
    w = f64(bf(w)).reshape(k // 32, 32, n)
    amax = np.abs(w).max(1)
    if fmt == "e4m3":
        byte = np.frexp(amax)[1] - 1 + 127 - 7
    else:
        mant, ex = np.frexp(amax / 6.0)
        byte = np.where(mant > 0.5, ex, ex - 1) + 127
    byte = np.clip(np.where(amax > 0, byte, 1), 1, 254)
    scaled = (w * np.exp2(127.0 - byte)[:, None, :]).reshape(k, n).astype(np.float32)
    by_word = np.ascontiguousarray(scaled.reshape(k // 512, 128, 4, n).transpose(0, 1, 3, 2))
    if fmt == "e4m3":
        words = by_word.astype(ml_dtypes.float8_e4m3fn).view(np.uint8)
    else:
        c = by_word.astype(ml_dtypes.float4_e2m1fn).view(np.uint8) & 0xF
        words = c[..., 0::2] | (c[..., 1::2] << 4)
    return np.ascontiguousarray(words), np.ascontiguousarray(byte.astype(np.uint8).reshape(k // 512, 16, n))


def unpack_weight(words, scales, fmt):
    g, p, n, _ = words.shape
    if fmt == "e4m3":
        vals = np.ascontiguousarray(words).view(ml_dtypes.float8_e4m3fn).astype(np.float64)
    else:
        nib = np.empty((g, p, n, 4), np.uint8)
        nib[..., 0::2] = words & 0xF
        nib[..., 1::2] = words >> 4
        vals = E2M1[nib]
    vals = vals * np.repeat(np.exp2(scales.astype(np.float64) - 127.0), 8, axis=1)[..., None]
    return vals.transpose(0, 1, 3, 2).reshape(g * 512, n)

def pack4(w):
    words, scales = pack_weight(w, "e2m1")
    return words.reshape(words.shape[0], 128, -1), scales


def unpack4(words, scales):
    return unpack_weight(words.reshape(words.shape[0], 128, -1, 2), scales, "e2m1")


B, I, H = 1024, 2048, 256


def sigmoid(v):
    return 1.0 / (1.0 + np.exp(-v))


def setup_inputs():
    s = mx_kscale(I)
    input_ = bf(np.random.standard_normal((B, I)) * s)
    c_input = bf(np.random.standard_normal((B, 1, H)))
    h_0 = bf(np.random.standard_normal((B, H)))
    weight_ih_words, weight_ih_scales = pack4(np.random.standard_normal((I, 3 * H)) / np.sqrt(I) / s[:, None])
    weight_hh = bf(np.random.standard_normal((H, 3 * H)) / np.sqrt(H))
    alpha_weight_ih_words, alpha_weight_ih_scales = pack4(np.random.standard_normal((I, H)) / np.sqrt(I) / s[:, None])
    alpha_weight_hh = bf(np.random.standard_normal((H, H)) / np.sqrt(H))
    bias = bf(np.random.standard_normal(3 * H) * 0.5)
    alpha_bias = bf(np.random.standard_normal(H) * 0.5)
    return {
        "input_": input_,
        "c_input": c_input,
        "h_0": h_0,
        "weight_ih_words": weight_ih_words,
        "weight_ih_scales": weight_ih_scales,
        "weight_hh": weight_hh,
        "alpha_weight_ih_words": alpha_weight_ih_words,
        "alpha_weight_ih_scales": alpha_weight_ih_scales,
        "alpha_weight_hh": alpha_weight_hh,
        "bias": bias,
        "alpha_bias": alpha_bias,
    }


def reference(input_, c_input, h_0, weight_ih_words, weight_ih_scales, weight_hh, alpha_weight_ih_words, alpha_weight_ih_scales, alpha_weight_hh, bias, alpha_bias):
    xq = mxq(f64(input_), 1, "e4m3")
    wh_b = f64(h_0) @ f64(weight_hh) + f64(bias)
    wi = xq @ unpack4(weight_ih_words, weight_ih_scales)
    pre = wh_b + wi
    i_gate = sigmoid(pre[:, :H])
    o_gate = sigmoid(pre[:, H:2 * H])
    g = np.tanh(pre[:, 2 * H:])
    c_in = f64(c_input)[:, 0, :]
    alpha = sigmoid((xq @ unpack4(alpha_weight_ih_words, alpha_weight_ih_scales)) + f64(alpha_bias) + c_in @ f64(alpha_weight_hh))
    e_i = np.exp(i_gate)
    e_a = np.exp(alpha)
    denom = e_i + e_a
    w_i = e_i / denom
    w_a = e_a / denom
    c_1 = w_i * g + w_a * c_in
    h_1 = o_gate * np.tanh(c_1)
    return (h_1, c_1)

@@ -1,0 +1,315 @@
+from contextlib import ExitStack
+
+import concourse.mybir as mybir
+from concourse.masks import make_identity
+
+F32 = mybir.dt.float32
+BF16 = mybir.dt.bfloat16
+I32 = mybir.dt.int32
+U32 = mybir.dt.uint32
+U8 = mybir.dt.uint8
+FP8X4 = mybir.dt.float8_e4m3fn_x4
+FP4X4 = mybir.dt.float4_e2m1fn_x4
+ACT = mybir.ActivationFunctionType
+ALU = mybir.AluOpType
+
+P = 128
+B, I, H = 1024, 2048, 256
+ROW_TILES = B // P
+K_PASS = 4 * P
+PASSES = I // K_PASS
+K_CHUNKS = H // P
+GATES = 4 * H
+BANK = 512
+A0, I0, O0, G0 = 0, H, 2 * H, 3 * H
+LOOKAHEAD = 2
+
+FLOPS = 2 * B * I * GATES + 2 * B * H * GATES
+
+
+def tile_multiinputlstmcell_pa_kernel(
+    tc,
+    input_,
+    c_input,
+    h_0,
+    weight_ih_words,
+    weight_ih_scales,
+    weight_hh,
+    alpha_weight_ih_words,
+    alpha_weight_ih_scales,
+    alpha_weight_hh,
+    bias,
+    alpha_bias,
+    out_0,
+    out_1,
+):
+    nc = tc.nc
+    with ExitStack() as ctx:
+        keep = ctx.enter_context(tc.tile_pool(name="keep", bufs=1))
+        work = ctx.enter_context(tc.tile_pool(name="work", bufs=3))
+        long_lived = ctx.enter_context(tc.tile_pool(name="long_lived", bufs=LOOKAHEAD + 2))
+        ps_t = ctx.enter_context(tc.psum_pool(name="ps_t", bufs=2))
+        ps_plain = ctx.enter_context(tc.psum_pool(name="ps_plain", bufs=2))
+        ps_mx = ctx.enter_context(tc.psum_pool(name="ps_mx", bufs=4))
+        ctx.enter_context(tc.manual_schedule())
+
+        x_rows = input_.rearrange("(p r) k -> p r k", r=ROW_TILES)
+        h_rows = h_0.rearrange("(p r) k -> p r k", r=ROW_TILES)
+        c_rows = c_input.rearrange("(p r) o k -> p r (o k)", r=ROW_TILES)
+        h1_rows = out_0.rearrange("(p r) n -> p r n", r=ROW_TILES)
+        c1_rows = out_1.rearrange("(p r) n -> p r n", r=ROW_TILES)
+
+        x_sb = keep.tile([P, ROW_TILES, I], BF16)
+        h_sb = keep.tile([P, ROW_TILES, H], BF16)
+        c_sb = keep.tile([P, ROW_TILES, H], BF16)
+        w_plain = keep.tile([P, K_CHUNKS, GATES], BF16)
+        w_words = keep.tile([P, PASSES, 2 * GATES], U8, align_bytes=64)
+        w_planes = keep.tile([P, PASSES, GATES], U8, align_bytes=64)
+        x_codes = keep.tile([P, ROW_TILES, PASSES * P], U32, align_bytes=64)
+        x_planes = keep.tile([P, ROW_TILES, PASSES * P], U8, align_bytes=64)
+        hT = keep.tile([P, ROW_TILES, K_CHUNKS, P], BF16)
+        cT = keep.tile([P, ROW_TILES, K_CHUNKS, P], BF16)
+        ident_f32 = keep.tile([P, P], F32)
+        ident_bf = keep.tile([P, P], BF16)
+        ones = keep.tile([P, P], BF16)
+        bias_rows = keep.tile([P, GATES], BF16)
+        bias_all = keep.tile([P, GATES], F32)
+        table_in = keep.tile([P, 1], F32)
+        table_out = keep.tile([P, 1], F32)
+
+        nc.vector.memset(w_planes[:].bitcast(I32), 0)
+        nc.vector.memset(bias_rows[:], 0.0)
+        nc.vector.memset(ones[:], 1.0)
+        nc.vector.memset(table_in[:], 0.0)
+        nc.scalar.activation(out=table_out[:], in_=table_in[:], func=ACT.Sigmoid)
+        make_identity(nc, ident_bf[:])
+        make_identity(nc, ident_f32[:])
+
+        nc.sync.dma_start(out=h_sb[:], in_=h_rows)
+        nc.sync.dma_start(out=c_sb[:], in_=c_rows)
+        nc.sync.dma_start(
+            out=w_plain[:, :, A0:I0], in_=alpha_weight_hh.rearrange("(c p) n -> p c n", p=P)
+        )
+        nc.sync.dma_start(
+            out=w_plain[:, :, I0:GATES], in_=weight_hh.rearrange("(c p) n -> p c n", p=P)
+        )
+        nc.sync.dma_start(out=bias_rows[0:1, A0:I0], in_=alpha_bias.unsqueeze(0))
+        nc.sync.dma_start(out=bias_rows[0:1, I0:GATES], in_=bias.unsqueeze(0))
+        for r in range(2):
+            nc.sync.dma_start(out=x_sb[:, r, :], in_=x_rows[:, r, :])
+        for j in range(4):
+            nc.sync.dma_start(
+                out=w_planes[j:P:32, :, A0:I0].bitcast(I32),
+                in_=alpha_weight_ih_scales[:, j:16:4, :].rearrange("g q n -> q g n").bitcast(I32),
+            )
+            nc.sync.dma_start(
+                out=w_planes[j:P:32, :, I0:GATES].bitcast(I32),
+                in_=weight_ih_scales[:, j:16:4, :].rearrange("g q n -> q g n").bitcast(I32),
+            )
+        nc.sync.dma_start(
+            out=w_words[:, :, 2 * A0 : 2 * I0].bitcast(I32),
+            in_=alpha_weight_ih_words.rearrange("g p b -> p g b").bitcast(I32),
+        )
+        nc.sync.dma_start(
+            out=w_words[:, :, 2 * I0 : 2 * GATES].bitcast(I32),
+            in_=weight_ih_words.rearrange("g p b -> p g b").bitcast(I32),
+        )
+        for r in range(2, ROW_TILES):
+            nc.sync.dma_start(out=x_sb[:, r, :], in_=x_rows[:, r, :])
+
+        for state_sb, stateT in ((h_sb, hT), (c_sb, cT)):
+            for pair in range(ROW_TILES // 2):
+                st_ps = ps_t.tile([P, 2, K_CHUNKS, P], BF16, tag="transposed")
+                for n in range(2):
+                    for c in range(K_CHUNKS):
+                        nc.tensor.transpose(
+                            st_ps[:, n, c, :],
+                            state_sb[:, 2 * pair + n, c * P : (c + 1) * P],
+                            ident_bf[:],
+                        )
+                nc.scalar.copy(out=stateT[:, 2 * pair : 2 * pair + 2, :, :], in_=st_ps[:])
+
+        for bank in range(GATES // BANK):
+            cols = slice(bank * BANK, (bank + 1) * BANK)
+            bias_ps = ps_plain.tile([P, BANK], F32, tag="plain")
+            nc.tensor.matmul(bias_ps[:], lhsT=ones[:], rhs=bias_rows[:, cols], start=True, stop=True)
+            nc.vector.tensor_copy(out=bias_all[:, cols], in_=bias_ps[:])
+
+        row_tiles = range(ROW_TILES)
+        xt = {}
+        sums = {}
+        grouped = {}
+        plain_sb = {}
+        acc = {}
+        pre = {}
+        gates = {}
+        i_minus_a = {}
+        w_i = {}
+        g_minus_c = {}
+        c_1 = {}
+        tanh_c = {}
+
+        def weave(r):
+            if r not in row_tiles:
+                return
+            x_words = x_sb[:, r, :].bitcast(F32)
+            xt_lo = ps_t.tile([P, 2, 2, P], F32, tag="transposed")
+            xt_hi = ps_t.tile([P, 2, 2, P], F32, tag="transposed")
+            xt[r] = (xt_lo, xt_hi)
+            sum_ai = ps_plain.tile([P, BANK], F32, tag="plain")
+            sum_og = ps_plain.tile([P, BANK], F32, tag="plain")
+            sums[r] = (sum_ai, sum_og)
+            products = (
+                (sum_ai[:, 0:H], cT, A0, H),
+                (sum_ai[:, H:BANK], hT, I0, H),
+                (sum_og[:], hT, O0, 2 * H),
+            )
+            turned = 0
+            for out_cols, stateT, first, width in products:
+                for c in range(K_CHUNKS):
+                    nc.tensor.matmul(
+                        out_cols,
+                        lhsT=stateT[:, r, c, :],
+                        rhs=w_plain[:, c, first : first + width],
+                        start=(c == 0),
+                        stop=(c == K_CHUNKS - 1),
+                    )
+                    for n in range(width // H):
+                        g, u = turned // 2, turned % 2
+                        nc.tensor.transpose(
+                            xt[r][g // 2][:, g % 2, u, :],
+                            x_words[:, 256 * g + u : 256 * (g + 1) : 2],
+                            ident_f32[:],
+                        )
+                        turned += 1
+
+        def x_out(r, half):
+            if r not in row_tiles:
+                return
+            if half == 0:
+                grouped[r] = work.tile([P, PASSES, P, 4], BF16, align_bytes=64, name="grouped")
+            nc.scalar.copy(
+                out=grouped[r][:].bitcast(F32)[:, 2 * half : 2 * half + 2, :, :],
+                in_=xt[r][half][:].rearrange("p g u r -> p g r u"),
+            )
+
+        def plain_out(r, bank):
+            if r not in row_tiles:
+                return
+            if bank == 0:
+                plain_sb[r] = long_lived.tile([P, GATES], F32, name="plain_sb")
+            cols = slice(bank * BANK, (bank + 1) * BANK)
+            nc.vector.tensor_tensor(
+                out=plain_sb[r][:, cols], in0=sums[r][bank][:], in1=bias_all[:, cols], op=ALU.add
+            )
+
+        def quantise(r):
+            if r not in row_tiles:
+                return
+            nc.vector.quantize_mx(
+                out=x_codes[:, r, :].bitcast(FP8X4),
+                scales=x_planes[:, r, :],
+                in_=grouped[r][:].rearrange("p g r t -> p (g r t)"),
+            )
+
+        def mx_passes(r, bank):
+            if r not in row_tiles:
+                return
+            acc[(r, bank)] = ps_mx.tile([P, BANK], F32, tag="mx", name="acc")
+            for g in range(PASSES):
+                rows = slice(g * P, (g + 1) * P)
+                nc.tensor.matmul_mx(
+                    out=acc[(r, bank)][:],
+                    lhsT=x_codes[:, r, rows].bitcast(FP8X4),
+                    lhsT_scale=x_planes[:, r, rows],
+                    rhs=w_words[:, g, 2 * bank * BANK : 2 * (bank + 1) * BANK].bitcast(FP4X4),
+                    rhs_scale=w_planes[:, g, bank * BANK : (bank + 1) * BANK],
+                    start=(g == 0),
+                    stop=(g == PASSES - 1),
+                )
+
+        def add_plain(r, bank):
+            if r not in row_tiles:
+                return
+            if bank == 0:
+                pre[r] = work.tile([P, GATES], F32, name="pre")
+            cols = slice(bank * BANK, (bank + 1) * BANK)
+            nc.vector.tensor_tensor(
+                out=pre[r][:, cols], in0=acc[(r, bank)][:], in1=plain_sb[r][:, cols], op=ALU.add
+            )
+
+        def sigmoid_ai(r):
+            if r not in row_tiles:
+                return
+            gates[r] = long_lived.tile([P, GATES], F32, name="gates")
+            nc.scalar.activation(out=gates[r][:, A0:O0], in_=pre[r][:, A0:O0], func=ACT.Sigmoid)
+
+        def sigmoid_o_tanh_g(r):
+            if r not in row_tiles:
+                return
+            nc.scalar.activation(out=gates[r][:, G0:GATES], in_=pre[r][:, G0:GATES], func=ACT.Tanh)
+            nc.scalar.activation(out=gates[r][:, O0:G0], in_=pre[r][:, O0:G0], func=ACT.Sigmoid)
+
+        def subtract_a(r):
+            if r not in row_tiles:
+                return
+            i_minus_a[r] = work.tile([P, H], F32, name="i_minus_a")
+            nc.vector.tensor_tensor(
+                out=i_minus_a[r][:], in0=gates[r][:, I0:O0], in1=gates[r][:, A0:I0], op=ALU.subtract
+            )
+
+        def softmax_weight(r):
+            if r not in row_tiles:
+                return
+            w_i[r] = work.tile([P, H], F32, name="w_i")
+            nc.scalar.activation(out=w_i[r][:], in_=i_minus_a[r][:], func=ACT.Sigmoid)
+
+        def subtract_c(r):
+            if r not in row_tiles:
+                return
+            g_minus_c[r] = work.tile([P, H], F32, name="g_minus_c")
+            nc.vector.tensor_tensor(
+                out=g_minus_c[r][:], in0=gates[r][:, G0:GATES], in1=c_sb[:, r, :], op=ALU.subtract
+            )
+
+        def new_cell(r):
+            if r not in row_tiles:
+                return
+            step = work.tile([P, H], F32, name="step")
+            nc.vector.tensor_tensor(out=step[:], in0=w_i[r][:], in1=g_minus_c[r][:], op=ALU.mult)
+            c_1[r] = work.tile([P, H], F32, name="c_1")
+            nc.vector.tensor_tensor(out=c_1[r][:], in0=step[:], in1=c_sb[:, r, :], op=ALU.add)
+            nc.sync.dma_start(out=c1_rows[:, r, :], in_=c_1[r][:])
+
+        def tanh_of_cell(r):
+            if r not in row_tiles:
+                return
+            tanh_c[r] = work.tile([P, H], F32, name="tanh_c")
+            nc.scalar.activation(out=tanh_c[r][:], in_=c_1[r][:], func=ACT.Tanh)
+
+        def new_hidden(r):
+            if r not in row_tiles:
+                return
+            h_1 = work.tile([P, H], F32, name="h_1")
+            nc.vector.tensor_tensor(out=h_1[:], in0=gates[r][:, O0:G0], in1=tanh_c[r][:], op=ALU.mult)
+            nc.sync.dma_start(out=h1_rows[:, r, :], in_=h_1[:])
+
+        for p in range(-LOOKAHEAD, ROW_TILES + 2):
+            weave(p + LOOKAHEAD)
+            add_plain(p - 1, 1)
+            tanh_of_cell(p - 2)
+            x_out(p + LOOKAHEAD, 0)
+            plain_out(p + LOOKAHEAD, 0)
+            plain_out(p + LOOKAHEAD, 1)
+            subtract_a(p - 1)
+            sigmoid_o_tanh_g(p - 1)
+            new_hidden(p - 2)
+            softmax_weight(p - 1)
+            subtract_c(p - 1)
+            x_out(p + LOOKAHEAD, 1)
+            quantise(p + LOOKAHEAD - 1)
+            mx_passes(p, 0)
+            add_plain(p, 0)
+            sigmoid_ai(p)
+            new_cell(p - 1)
+            mx_passes(p, 1)

@@ -254,7 +254,7 @@ def tile_multiinputlstmcell_pa_kernel(
             if r not in row_tiles:
                 return
             i_minus_a[r] = work.tile([P, H], F32, name="i_minus_a")
-            nc.vector.tensor_tensor(
+            nc.gpsimd.tensor_tensor(
                 out=i_minus_a[r][:], in0=gates[r][:, I0:O0], in1=gates[r][:, A0:I0], op=ALU.subtract
             )
 
@@ -268,7 +268,7 @@ def tile_multiinputlstmcell_pa_kernel(
             if r not in row_tiles:
                 return
             g_minus_c[r] = work.tile([P, H], F32, name="g_minus_c")
-            nc.vector.tensor_tensor(
+            nc.gpsimd.tensor_tensor(
                 out=g_minus_c[r][:], in0=gates[r][:, G0:GATES], in1=c_sb[:, r, :], op=ALU.subtract
             )
 

@@ -95,7 +95,7 @@ def tile_multiinputlstmcell_pa_kernel(
         )
         nc.sync.dma_start(out=bias_rows[0:1, A0:I0], in_=alpha_bias.unsqueeze(0))
         nc.sync.dma_start(out=bias_rows[0:1, I0:GATES], in_=bias.unsqueeze(0))
-        for r in range(2):
+        for r in range(LOOKAHEAD + 1):
             nc.sync.dma_start(out=x_sb[:, r, :], in_=x_rows[:, r, :])
         for j in range(4):
             nc.sync.dma_start(
@@ -114,12 +114,12 @@ def tile_multiinputlstmcell_pa_kernel(
             out=w_words[:, :, 2 * I0 : 2 * GATES].bitcast(I32),
             in_=weight_ih_words.rearrange("g p b -> p g b").bitcast(I32),
         )
-        for r in range(2, ROW_TILES):
+        for r in range(LOOKAHEAD + 1, ROW_TILES):
             nc.sync.dma_start(out=x_sb[:, r, :], in_=x_rows[:, r, :])
 
         for state_sb, stateT in ((h_sb, hT), (c_sb, cT)):
             for pair in range(ROW_TILES // 2):
-                st_ps = ps_t.tile([P, 2, K_CHUNKS, P], BF16, tag="transposed")
+                st_ps = ps_mx.tile([P, 2, K_CHUNKS, P], BF16, tag="mx")
                 for n in range(2):
                     for c in range(K_CHUNKS):
                         nc.tensor.transpose(
@@ -127,7 +127,7 @@ def tile_multiinputlstmcell_pa_kernel(
                             state_sb[:, 2 * pair + n, c * P : (c + 1) * P],
                             ident_bf[:],
                         )
-                nc.scalar.copy(out=stateT[:, 2 * pair : 2 * pair + 2, :, :], in_=st_ps[:])
+                nc.vector.tensor_copy(out=stateT[:, 2 * pair : 2 * pair + 2, :, :], in_=st_ps[:])
 
         for bank in range(GATES // BANK):
             cols = slice(bank * BANK, (bank + 1) * BANK)
@@ -136,6 +136,7 @@ def tile_multiinputlstmcell_pa_kernel(
             nc.vector.tensor_copy(out=bias_all[:, cols], in_=bias_ps[:])
 
         row_tiles = range(ROW_TILES)
+        x_sorted = {}
         xt = {}
         sums = {}
         grouped = {}
@@ -146,13 +147,22 @@ def tile_multiinputlstmcell_pa_kernel(
         i_minus_a = {}
         w_i = {}
         g_minus_c = {}
+        step = {}
         c_1 = {}
         tanh_c = {}
+
+        def sort_words(r, half):
+            if r not in row_tiles:
+                return
+            if half == 0:
+                x_sorted[r] = work.tile([P, PASSES, 2, P], F32, name="x_sorted")
+            passes = slice(2 * half, 2 * half + 2)
+            x_words = x_sb[:, r, :].bitcast(F32).rearrange("p (g j u) -> p g u j", g=PASSES, u=2)
+            nc.scalar.copy(out=x_sorted[r][:, passes, :, :], in_=x_words[:, passes, :, :])
 
         def weave(r):
             if r not in row_tiles:
                 return
-            x_words = x_sb[:, r, :].bitcast(F32)
             xt_lo = ps_t.tile([P, 2, 2, P], F32, tag="transposed")
             xt_hi = ps_t.tile([P, 2, 2, P], F32, tag="transposed")
             xt[r] = (xt_lo, xt_hi)
@@ -178,7 +188,7 @@ def tile_multiinputlstmcell_pa_kernel(
                         g, u = turned // 2, turned % 2
                         nc.tensor.transpose(
                             xt[r][g // 2][:, g % 2, u, :],
-                            x_words[:, 256 * g + u : 256 * (g + 1) : 2],
+                            x_sorted[r][:, g, u, :],
                             ident_f32[:],
                         )
                         turned += 1
@@ -244,17 +254,24 @@ def tile_multiinputlstmcell_pa_kernel(
             gates[r] = long_lived.tile([P, GATES], F32, name="gates")
             nc.scalar.activation(out=gates[r][:, A0:O0], in_=pre[r][:, A0:O0], func=ACT.Sigmoid)
 
-        def sigmoid_o_tanh_g(r):
+        def tanh_g(r):
             if r not in row_tiles:
                 return
             nc.scalar.activation(out=gates[r][:, G0:GATES], in_=pre[r][:, G0:GATES], func=ACT.Tanh)
+
+        def sigmoid_o(r):
+            if r not in row_tiles:
+                return
             nc.scalar.activation(out=gates[r][:, O0:G0], in_=pre[r][:, O0:G0], func=ACT.Sigmoid)
+
+        def subtracter(r):
+            return nc.vector if r == ROW_TILES - 1 else nc.gpsimd
 
         def subtract_a(r):
             if r not in row_tiles:
                 return
             i_minus_a[r] = work.tile([P, H], F32, name="i_minus_a")
-            nc.gpsimd.tensor_tensor(
+            subtracter(r).tensor_tensor(
                 out=i_minus_a[r][:], in0=gates[r][:, I0:O0], in1=gates[r][:, A0:I0], op=ALU.subtract
             )
 
@@ -268,17 +285,21 @@ def tile_multiinputlstmcell_pa_kernel(
             if r not in row_tiles:
                 return
             g_minus_c[r] = work.tile([P, H], F32, name="g_minus_c")
-            nc.gpsimd.tensor_tensor(
+            subtracter(r).tensor_tensor(
                 out=g_minus_c[r][:], in0=gates[r][:, G0:GATES], in1=c_sb[:, r, :], op=ALU.subtract
             )
+
+        def weighted_step(r):
+            if r not in row_tiles:
+                return
+            step[r] = work.tile([P, H], F32, name="step")
+            nc.vector.tensor_tensor(out=step[r][:], in0=w_i[r][:], in1=g_minus_c[r][:], op=ALU.mult)
 
         def new_cell(r):
             if r not in row_tiles:
                 return
-            step = work.tile([P, H], F32, name="step")
-            nc.vector.tensor_tensor(out=step[:], in0=w_i[r][:], in1=g_minus_c[r][:], op=ALU.mult)
             c_1[r] = work.tile([P, H], F32, name="c_1")
-            nc.vector.tensor_tensor(out=c_1[r][:], in0=step[:], in1=c_sb[:, r, :], op=ALU.add)
+            nc.vector.tensor_tensor(out=c_1[r][:], in0=step[r][:], in1=c_sb[:, r, :], op=ALU.add)
             nc.sync.dma_start(out=c1_rows[:, r, :], in_=c_1[r][:])
 
         def tanh_of_cell(r):
@@ -294,22 +315,26 @@ def tile_multiinputlstmcell_pa_kernel(
             nc.vector.tensor_tensor(out=h_1[:], in0=gates[r][:, O0:G0], in1=tanh_c[r][:], op=ALU.mult)
             nc.sync.dma_start(out=h1_rows[:, r, :], in_=h_1[:])
 
-        for p in range(-LOOKAHEAD, ROW_TILES + 2):
-            weave(p + LOOKAHEAD)
+        for p in range(-LOOKAHEAD - 1, ROW_TILES + 3):
             add_plain(p - 1, 1)
-            tanh_of_cell(p - 2)
-            x_out(p + LOOKAHEAD, 0)
-            plain_out(p + LOOKAHEAD, 0)
-            plain_out(p + LOOKAHEAD, 1)
             subtract_a(p - 1)
-            sigmoid_o_tanh_g(p - 1)
-            new_hidden(p - 2)
+            sort_words(p + LOOKAHEAD + 1, 0)
+            tanh_g(p - 1)
+            weave(p + LOOKAHEAD)
+            mx_passes(p, 0)
+            quantise(p + LOOKAHEAD - 1)
+            mx_passes(p, 1)
+            plain_out(p + LOOKAHEAD, 0)
+            sort_words(p + LOOKAHEAD + 1, 1)
+            new_cell(p - 2)
+            plain_out(p + LOOKAHEAD, 1)
             softmax_weight(p - 1)
+            new_hidden(p - 3)
+            x_out(p + LOOKAHEAD, 0)
             subtract_c(p - 1)
             x_out(p + LOOKAHEAD, 1)
-            quantise(p + LOOKAHEAD - 1)
-            mx_passes(p, 0)
             add_plain(p, 0)
             sigmoid_ai(p)
-            new_cell(p - 1)
-            mx_passes(p, 1)
+            tanh_of_cell(p - 2)
+            weighted_step(p - 1)
+            sigmoid_o(p - 1)

@@ -136,7 +136,6 @@ def tile_multiinputlstmcell_pa_kernel(
             nc.vector.tensor_copy(out=bias_all[:, cols], in_=bias_ps[:])
 
         row_tiles = range(ROW_TILES)
-        x_sorted = {}
         xt = {}
         sums = {}
         grouped = {}
@@ -151,18 +150,10 @@ def tile_multiinputlstmcell_pa_kernel(
         c_1 = {}
         tanh_c = {}
 
-        def sort_words(r, half):
-            if r not in row_tiles:
-                return
-            if half == 0:
-                x_sorted[r] = work.tile([P, PASSES, 2, P], F32, name="x_sorted")
-            passes = slice(2 * half, 2 * half + 2)
-            x_words = x_sb[:, r, :].bitcast(F32).rearrange("p (g j u) -> p g u j", g=PASSES, u=2)
-            nc.scalar.copy(out=x_sorted[r][:, passes, :, :], in_=x_words[:, passes, :, :])
-
         def weave(r):
             if r not in row_tiles:
                 return
+            x_words = x_sb[:, r, :].bitcast(F32)
             xt_lo = ps_t.tile([P, 2, 2, P], F32, tag="transposed")
             xt_hi = ps_t.tile([P, 2, 2, P], F32, tag="transposed")
             xt[r] = (xt_lo, xt_hi)
@@ -188,7 +179,7 @@ def tile_multiinputlstmcell_pa_kernel(
                         g, u = turned // 2, turned % 2
                         nc.tensor.transpose(
                             xt[r][g // 2][:, g % 2, u, :],
-                            x_sorted[r][:, g, u, :],
+                            x_words[:, 256 * g + u : 256 * (g + 1) : 2],
                             ident_f32[:],
                         )
                         turned += 1
@@ -315,17 +306,15 @@ def tile_multiinputlstmcell_pa_kernel(
             nc.vector.tensor_tensor(out=h_1[:], in0=gates[r][:, O0:G0], in1=tanh_c[r][:], op=ALU.mult)
             nc.sync.dma_start(out=h1_rows[:, r, :], in_=h_1[:])
 
-        for p in range(-LOOKAHEAD - 1, ROW_TILES + 3):
+        for p in range(-LOOKAHEAD, ROW_TILES + 3):
             add_plain(p - 1, 1)
             subtract_a(p - 1)
-            sort_words(p + LOOKAHEAD + 1, 0)
             tanh_g(p - 1)
             weave(p + LOOKAHEAD)
             mx_passes(p, 0)
             quantise(p + LOOKAHEAD - 1)
             mx_passes(p, 1)
             plain_out(p + LOOKAHEAD, 0)
-            sort_words(p + LOOKAHEAD + 1, 1)
             new_cell(p - 2)
             plain_out(p + LOOKAHEAD, 1)
             softmax_weight(p - 1)

@@ -48,9 +48,7 @@ def tile_multiinputlstmcell_pa_kernel(
         keep = ctx.enter_context(tc.tile_pool(name="keep", bufs=1))
         work = ctx.enter_context(tc.tile_pool(name="work", bufs=3))
         long_lived = ctx.enter_context(tc.tile_pool(name="long_lived", bufs=LOOKAHEAD + 2))
-        ps_t = ctx.enter_context(tc.psum_pool(name="ps_t", bufs=2))
-        ps_plain = ctx.enter_context(tc.psum_pool(name="ps_plain", bufs=2))
-        ps_mx = ctx.enter_context(tc.psum_pool(name="ps_mx", bufs=4))
+        psum = ctx.enter_context(tc.psum_pool(name="psum", bufs=8))
         ctx.enter_context(tc.manual_schedule())
 
         x_rows = input_.rearrange("(p r) k -> p r k", r=ROW_TILES)
@@ -85,19 +83,10 @@ def tile_multiinputlstmcell_pa_kernel(
         make_identity(nc, ident_bf[:])
         make_identity(nc, ident_f32[:])
 
-        nc.sync.dma_start(out=h_sb[:], in_=h_rows)
-        nc.sync.dma_start(out=c_sb[:], in_=c_rows)
-        nc.sync.dma_start(
-            out=w_plain[:, :, A0:I0], in_=alpha_weight_hh.rearrange("(c p) n -> p c n", p=P)
-        )
-        nc.sync.dma_start(
-            out=w_plain[:, :, I0:GATES], in_=weight_hh.rearrange("(c p) n -> p c n", p=P)
-        )
-        nc.sync.dma_start(out=bias_rows[0:1, A0:I0], in_=alpha_bias.unsqueeze(0))
-        nc.sync.dma_start(out=bias_rows[0:1, I0:GATES], in_=bias.unsqueeze(0))
-        for r in range(LOOKAHEAD + 1):
+        def load_x(r):
             nc.sync.dma_start(out=x_sb[:, r, :], in_=x_rows[:, r, :])
-        for j in range(4):
+
+        def load_scales(j):
             nc.sync.dma_start(
                 out=w_planes[j:P:32, :, A0:I0].bitcast(I32),
                 in_=alpha_weight_ih_scales[:, j:16:4, :].rearrange("g q n -> q g n").bitcast(I32),
@@ -106,20 +95,47 @@ def tile_multiinputlstmcell_pa_kernel(
                 out=w_planes[j:P:32, :, I0:GATES].bitcast(I32),
                 in_=weight_ih_scales[:, j:16:4, :].rearrange("g q n -> q g n").bitcast(I32),
             )
-        nc.sync.dma_start(
-            out=w_words[:, :, 2 * A0 : 2 * I0].bitcast(I32),
-            in_=alpha_weight_ih_words.rearrange("g p b -> p g b").bitcast(I32),
-        )
-        nc.sync.dma_start(
-            out=w_words[:, :, 2 * I0 : 2 * GATES].bitcast(I32),
-            in_=weight_ih_words.rearrange("g p b -> p g b").bitcast(I32),
-        )
-        for r in range(LOOKAHEAD + 1, ROW_TILES):
-            nc.sync.dma_start(out=x_sb[:, r, :], in_=x_rows[:, r, :])
+
+        def load_words():
+            nc.sync.dma_start(
+                out=w_words[:, :, 2 * A0 : 2 * I0].bitcast(I32),
+                in_=alpha_weight_ih_words.rearrange("g p b -> p g b").bitcast(I32),
+            )
+            nc.sync.dma_start(
+                out=w_words[:, :, 2 * I0 : 2 * GATES].bitcast(I32),
+                in_=weight_ih_words.rearrange("g p b -> p g b").bitcast(I32),
+            )
+
+        def load_plain():
+            nc.sync.dma_start(
+                out=w_plain[:, :, A0:I0], in_=alpha_weight_hh.rearrange("(c p) n -> p c n", p=P)
+            )
+            nc.sync.dma_start(
+                out=w_plain[:, :, I0:GATES], in_=weight_hh.rearrange("(c p) n -> p c n", p=P)
+            )
+
+        def load_bias():
+            nc.sync.dma_start(out=bias_rows[0:1, A0:I0], in_=alpha_bias.unsqueeze(0))
+            nc.sync.dma_start(out=bias_rows[0:1, I0:GATES], in_=bias.unsqueeze(0))
+
+        nc.sync.dma_start(out=h_sb[:], in_=h_rows)
+        load_scales(0)
+        nc.sync.dma_start(out=c_sb[:], in_=c_rows)
+        load_scales(1)
+        load_plain()
+        load_bias()
+        load_x(0)
+        load_scales(2)
+        load_x(1)
+        load_scales(3)
+        load_x(2)
+        load_words()
+        for r in range(3, ROW_TILES):
+            load_x(r)
 
         for state_sb, stateT in ((h_sb, hT), (c_sb, cT)):
             for pair in range(ROW_TILES // 2):
-                st_ps = ps_mx.tile([P, 2, K_CHUNKS, P], BF16, tag="mx")
+                st_ps = psum.tile([P, 2, K_CHUNKS, P], BF16, tag="bank")
                 for n in range(2):
                     for c in range(K_CHUNKS):
                         nc.tensor.transpose(
@@ -131,7 +147,7 @@ def tile_multiinputlstmcell_pa_kernel(
 
         for bank in range(GATES // BANK):
             cols = slice(bank * BANK, (bank + 1) * BANK)
-            bias_ps = ps_plain.tile([P, BANK], F32, tag="plain")
+            bias_ps = psum.tile([P, BANK], F32, tag="bank")
             nc.tensor.matmul(bias_ps[:], lhsT=ones[:], rhs=bias_rows[:, cols], start=True, stop=True)
             nc.vector.tensor_copy(out=bias_all[:, cols], in_=bias_ps[:])
 
@@ -154,11 +170,11 @@ def tile_multiinputlstmcell_pa_kernel(
             if r not in row_tiles:
                 return
             x_words = x_sb[:, r, :].bitcast(F32)
-            xt_lo = ps_t.tile([P, 2, 2, P], F32, tag="transposed")
-            xt_hi = ps_t.tile([P, 2, 2, P], F32, tag="transposed")
+            xt_lo = psum.tile([P, 2, 2, P], F32, tag="bank")
+            xt_hi = psum.tile([P, 2, 2, P], F32, tag="bank")
             xt[r] = (xt_lo, xt_hi)
-            sum_ai = ps_plain.tile([P, BANK], F32, tag="plain")
-            sum_og = ps_plain.tile([P, BANK], F32, tag="plain")
+            sum_ai = psum.tile([P, BANK], F32, tag="bank")
+            sum_og = psum.tile([P, BANK], F32, tag="bank")
             sums[r] = (sum_ai, sum_og)
             products = (
                 (sum_ai[:, 0:H], cT, A0, H),
@@ -216,7 +232,7 @@ def tile_multiinputlstmcell_pa_kernel(
         def mx_passes(r, bank):
             if r not in row_tiles:
                 return
-            acc[(r, bank)] = ps_mx.tile([P, BANK], F32, tag="mx", name="acc")
+            acc[(r, bank)] = psum.tile([P, BANK], F32, tag="bank", name="acc")
             for g in range(PASSES):
                 rows = slice(g * P, (g + 1) * P)
                 nc.tensor.matmul_mx(

@@ -161,7 +161,8 @@ def tile_multiinputlstmcell_pa_kernel(
         gates = {}
         i_minus_a = {}
         w_i = {}
-        g_minus_c = {}
+        w_a = {}
+        kept = {}
         step = {}
         c_1 = {}
         tanh_c = {}
@@ -255,6 +256,15 @@ def tile_multiinputlstmcell_pa_kernel(
                 out=pre[r][:, cols], in0=acc[(r, bank)][:], in1=plain_sb[r][:, cols], op=ALU.add
             )
 
+        def add_plain_gate(r, first):
+            cols = slice(first, first + H)
+            nc.vector.tensor_tensor(
+                out=pre[r][:, cols],
+                in0=acc[(r, 1)][:, first - BANK : first - BANK + H],
+                in1=plain_sb[r][:, cols],
+                op=ALU.add,
+            )
+
         def sigmoid_ai(r):
             if r not in row_tiles:
                 return
@@ -274,11 +284,11 @@ def tile_multiinputlstmcell_pa_kernel(
         def subtracter(r):
             return nc.vector if r == ROW_TILES - 1 else nc.gpsimd
 
-        def subtract_a(r):
+        def subtract_a(r, engine=None):
             if r not in row_tiles:
                 return
             i_minus_a[r] = work.tile([P, H], F32, name="i_minus_a")
-            subtracter(r).tensor_tensor(
+            (engine or subtracter(r)).tensor_tensor(
                 out=i_minus_a[r][:], in0=gates[r][:, I0:O0], in1=gates[r][:, A0:I0], op=ALU.subtract
             )
 
@@ -288,25 +298,29 @@ def tile_multiinputlstmcell_pa_kernel(
             w_i[r] = work.tile([P, H], F32, name="w_i")
             nc.scalar.activation(out=w_i[r][:], in_=i_minus_a[r][:], func=ACT.Sigmoid)
 
-        def subtract_c(r):
+        def keep_weight(r):
             if r not in row_tiles:
                 return
-            g_minus_c[r] = work.tile([P, H], F32, name="g_minus_c")
-            subtracter(r).tensor_tensor(
-                out=g_minus_c[r][:], in0=gates[r][:, G0:GATES], in1=c_sb[:, r, :], op=ALU.subtract
-            )
+            w_a[r] = work.tile([P, H], F32, name="w_a")
+            nc.scalar.activation(out=w_a[r][:], in_=i_minus_a[r][:], func=ACT.Sigmoid, scale=-1.0)
 
-        def weighted_step(r):
+        def kept_cell(r, engine=None):
+            if r not in row_tiles:
+                return
+            kept[r] = work.tile([P, H], F32, name="kept")
+            (engine or subtracter(r)).tensor_tensor(out=kept[r][:], in0=w_a[r][:], in1=c_sb[:, r, :], op=ALU.mult)
+
+        def new_part(r):
             if r not in row_tiles:
                 return
             step[r] = work.tile([P, H], F32, name="step")
-            nc.vector.tensor_tensor(out=step[r][:], in0=w_i[r][:], in1=g_minus_c[r][:], op=ALU.mult)
+            nc.vector.tensor_tensor(out=step[r][:], in0=w_i[r][:], in1=gates[r][:, G0:GATES], op=ALU.mult)
 
-        def new_cell(r):
+        def summed_cell(r):
             if r not in row_tiles:
                 return
             c_1[r] = work.tile([P, H], F32, name="c_1")
-            nc.vector.tensor_tensor(out=c_1[r][:], in0=step[r][:], in1=c_sb[:, r, :], op=ALU.add)
+            nc.vector.tensor_tensor(out=c_1[r][:], in0=step[r][:], in1=kept[r][:], op=ALU.add)
             nc.sync.dma_start(out=c1_rows[:, r, :], in_=c_1[r][:])
 
         def tanh_of_cell(r):
@@ -315,14 +329,16 @@ def tile_multiinputlstmcell_pa_kernel(
             tanh_c[r] = work.tile([P, H], F32, name="tanh_c")
             nc.scalar.activation(out=tanh_c[r][:], in_=c_1[r][:], func=ACT.Tanh)
 
-        def new_hidden(r):
+        def new_hidden(r, engine=None):
             if r not in row_tiles:
                 return
             h_1 = work.tile([P, H], F32, name="h_1")
-            nc.vector.tensor_tensor(out=h_1[:], in0=gates[r][:, O0:G0], in1=tanh_c[r][:], op=ALU.mult)
+            (engine or nc.gpsimd).tensor_tensor(
+                out=h_1[:], in0=gates[r][:, O0:G0], in1=tanh_c[r][:], op=ALU.mult
+            )
             nc.sync.dma_start(out=h1_rows[:, r, :], in_=h_1[:])
 
-        for p in range(-LOOKAHEAD, ROW_TILES + 3):
+        for p in range(-LOOKAHEAD, ROW_TILES - 2):
             add_plain(p - 1, 1)
             subtract_a(p - 1)
             tanh_g(p - 1)
@@ -331,15 +347,66 @@ def tile_multiinputlstmcell_pa_kernel(
             quantise(p + LOOKAHEAD - 1)
             mx_passes(p, 1)
             plain_out(p + LOOKAHEAD, 0)
-            new_cell(p - 2)
+            summed_cell(p - 2)
             plain_out(p + LOOKAHEAD, 1)
             softmax_weight(p - 1)
+            keep_weight(p - 1)
             new_hidden(p - 3)
             x_out(p + LOOKAHEAD, 0)
-            subtract_c(p - 1)
+            kept_cell(p - 1)
             x_out(p + LOOKAHEAD, 1)
             add_plain(p, 0)
             sigmoid_ai(p)
             tanh_of_cell(p - 2)
-            weighted_step(p - 1)
+            new_part(p - 1)
             sigmoid_o(p - 1)
+
+
+        quantise(7)
+        add_plain(5, 1)
+        subtract_a(5)
+        tanh_g(5)
+        mx_passes(6, 0)
+        mx_passes(7, 0)
+        mx_passes(6, 1)
+        mx_passes(7, 1)
+        summed_cell(4)
+        softmax_weight(5)
+        keep_weight(5)
+        new_hidden(3)
+        kept_cell(5)
+        add_plain(6, 0)
+        sigmoid_ai(6)
+        tanh_of_cell(4)
+        new_part(5)
+        add_plain(7, 0)
+        sigmoid_ai(7)
+        new_hidden(4)
+        subtract_a(6, nc.vector)
+        softmax_weight(6)
+        sigmoid_o(5)
+        add_plain_gate(6, G0)
+        tanh_g(6)
+        keep_weight(6)
+        summed_cell(5)
+        add_plain_gate(6, O0)
+        subtract_a(7, nc.vector)
+        softmax_weight(7)
+        keep_weight(7)
+        tanh_of_cell(5)
+        new_part(6)
+        kept_cell(6, nc.vector)
+        add_plain_gate(7, G0)
+        tanh_g(7)
+        sigmoid_o(6)
+        summed_cell(6)
+        kept_cell(7, nc.vector)
+        new_hidden(5)
+        tanh_of_cell(6)
+        new_part(7)
+        add_plain_gate(7, O0)
+        summed_cell(7)
+        sigmoid_o(7)
+        tanh_of_cell(7)
+        new_hidden(6, nc.vector)
+        new_hidden(7, nc.vector)

@@ -182,7 +182,13 @@ def tile_multiinputlstmcell_pa_kernel(
                 (sum_ai[:, H:BANK], hT, I0, H),
                 (sum_og[:], hT, O0, 2 * H),
             )
-            turned = 0
+            for turned in range(2 * PASSES):
+                g, u = turned // 2, turned % 2
+                nc.tensor.transpose(
+                    xt[r][g // 2][:, g % 2, u, :],
+                    x_words[:, 256 * g + u : 256 * (g + 1) : 2],
+                    ident_f32[:],
+                )
             for out_cols, stateT, first, width in products:
                 for c in range(K_CHUNKS):
                     nc.tensor.matmul(
@@ -192,14 +198,6 @@ def tile_multiinputlstmcell_pa_kernel(
                         start=(c == 0),
                         stop=(c == K_CHUNKS - 1),
                     )
-                    for n in range(width // H):
-                        g, u = turned // 2, turned % 2
-                        nc.tensor.transpose(
-                            xt[r][g // 2][:, g % 2, u, :],
-                            x_words[:, 256 * g + u : 256 * (g + 1) : 2],
-                            ident_f32[:],
-                        )
-                        turned += 1
 
         def x_out(r, half):
             if r not in row_tiles:

@@ -22,7 +22,9 @@ K_CHUNKS = H // P
 GATES = 4 * H
 BANK = 512
 A0, I0, O0, G0 = 0, H, 2 * H, 3 * H
-LOOKAHEAD = 2
+X_AHEAD = 2
+PLAIN_AHEAD = 3
+HALF = ROW_TILES // 2
 
 FLOPS = 2 * B * I * GATES + 2 * B * H * GATES
 
@@ -47,7 +49,7 @@ def tile_multiinputlstmcell_pa_kernel(
     with ExitStack() as ctx:
         keep = ctx.enter_context(tc.tile_pool(name="keep", bufs=1))
         work = ctx.enter_context(tc.tile_pool(name="work", bufs=3))
-        long_lived = ctx.enter_context(tc.tile_pool(name="long_lived", bufs=LOOKAHEAD + 2))
+        long_lived = ctx.enter_context(tc.tile_pool(name="long_lived", bufs=PLAIN_AHEAD + 2))
         psum = ctx.enter_context(tc.psum_pool(name="psum", bufs=8))
         ctx.enter_context(tc.manual_schedule())
 
@@ -65,8 +67,8 @@ def tile_multiinputlstmcell_pa_kernel(
         w_planes = keep.tile([P, PASSES, GATES], U8, align_bytes=64)
         x_codes = keep.tile([P, ROW_TILES, PASSES * P], U32, align_bytes=64)
         x_planes = keep.tile([P, ROW_TILES, PASSES * P], U8, align_bytes=64)
-        hT = keep.tile([P, ROW_TILES, K_CHUNKS, P], BF16)
-        cT = keep.tile([P, ROW_TILES, K_CHUNKS, P], BF16)
+        hT = keep.tile([P, ROW_TILES, P, K_CHUNKS], BF16)
+        cT = keep.tile([P, ROW_TILES, P, K_CHUNKS], BF16)
         ident_f32 = keep.tile([P, P], F32)
         ident_bf = keep.tile([P, P], BF16)
         ones = keep.tile([P, P], BF16)
@@ -106,50 +108,53 @@ def tile_multiinputlstmcell_pa_kernel(
                 in_=weight_ih_words.rearrange("g p b -> p g b").bitcast(I32),
             )
 
-        def load_plain():
-            nc.sync.dma_start(
-                out=w_plain[:, :, A0:I0], in_=alpha_weight_hh.rearrange("(c p) n -> p c n", p=P)
-            )
-            nc.sync.dma_start(
-                out=w_plain[:, :, I0:GATES], in_=weight_hh.rearrange("(c p) n -> p c n", p=P)
-            )
+        def load_state(state_sb, rows_view, half):
+            tiles = slice(half * HALF, (half + 1) * HALF)
+            nc.sync.dma_start(out=state_sb[:, tiles, :], in_=rows_view[:, tiles, :])
 
         def load_bias():
             nc.sync.dma_start(out=bias_rows[0:1, A0:I0], in_=alpha_bias.unsqueeze(0))
             nc.sync.dma_start(out=bias_rows[0:1, I0:GATES], in_=bias.unsqueeze(0))
 
-        nc.sync.dma_start(out=h_sb[:], in_=h_rows)
-        load_scales(0)
-        nc.sync.dma_start(out=c_sb[:], in_=c_rows)
-        load_scales(1)
-        load_plain()
+        load_state(c_sb, c_rows, 0)
+        nc.sync.dma_start(
+            out=w_plain[:, :, A0:I0], in_=alpha_weight_hh.rearrange("(p e) n -> p e n", e=K_CHUNKS)
+        )
+        load_state(h_sb, h_rows, 0)
+        nc.sync.dma_start(
+            out=w_plain[:, :, I0:GATES], in_=weight_hh.rearrange("(p e) n -> p e n", e=K_CHUNKS)
+        )
         load_bias()
         load_x(0)
-        load_scales(2)
+        load_scales(0)
         load_x(1)
-        load_scales(3)
+        load_scales(1)
         load_x(2)
+        load_scales(2)
+        load_state(h_sb, h_rows, 1)
+        load_scales(3)
         load_words()
+        load_state(c_sb, c_rows, 1)
         for r in range(3, ROW_TILES):
             load_x(r)
 
-        for state_sb, stateT in ((h_sb, hT), (c_sb, cT)):
-            for pair in range(ROW_TILES // 2):
-                st_ps = psum.tile([P, 2, K_CHUNKS, P], BF16, tag="bank")
-                for n in range(2):
-                    for c in range(K_CHUNKS):
-                        nc.tensor.transpose(
-                            st_ps[:, n, c, :],
-                            state_sb[:, 2 * pair + n, c * P : (c + 1) * P],
-                            ident_bf[:],
-                        )
-                nc.vector.tensor_copy(out=stateT[:, 2 * pair : 2 * pair + 2, :, :], in_=st_ps[:])
+        def turn_state(state_sb, stateT, half):
+            words_ps = psum.tile([P, HALF, P], F32, tag="bank", name="words_ps")
+            for n in range(HALF):
+                nc.tensor.transpose(
+                    words_ps[:, n, :], state_sb[:, half * HALF + n, :].bitcast(F32), ident_f32[:]
+                )
+            tiles = slice(half * HALF, (half + 1) * HALF)
+            nc.vector.tensor_copy(
+                out=stateT[:, tiles, :, :].rearrange("p n r e -> p n (r e)").bitcast(F32), in_=words_ps[:]
+            )
 
-        for bank in range(GATES // BANK):
-            cols = slice(bank * BANK, (bank + 1) * BANK)
-            bias_ps = psum.tile([P, BANK], F32, tag="bank")
-            nc.tensor.matmul(bias_ps[:], lhsT=ones[:], rhs=bias_rows[:, cols], start=True, stop=True)
-            nc.vector.tensor_copy(out=bias_all[:, cols], in_=bias_ps[:])
+        def spread_biases():
+            for bank in range(GATES // BANK):
+                cols = slice(bank * BANK, (bank + 1) * BANK)
+                bias_ps = psum.tile([P, BANK], F32, tag="bank", name="bias_ps")
+                nc.tensor.matmul(bias_ps[:], lhsT=ones[:], rhs=bias_rows[:, cols], start=True, stop=True)
+                nc.vector.tensor_copy(out=bias_all[:, cols], in_=bias_ps[:])
 
         row_tiles = range(ROW_TILES)
         xt = {}
@@ -167,21 +172,13 @@ def tile_multiinputlstmcell_pa_kernel(
         c_1 = {}
         tanh_c = {}
 
-        def weave(r):
+        def turn_x(r):
             if r not in row_tiles:
                 return
             x_words = x_sb[:, r, :].bitcast(F32)
             xt_lo = psum.tile([P, 2, 2, P], F32, tag="bank")
             xt_hi = psum.tile([P, 2, 2, P], F32, tag="bank")
             xt[r] = (xt_lo, xt_hi)
-            sum_ai = psum.tile([P, BANK], F32, tag="bank")
-            sum_og = psum.tile([P, BANK], F32, tag="bank")
-            sums[r] = (sum_ai, sum_og)
-            products = (
-                (sum_ai[:, 0:H], cT, A0, H),
-                (sum_ai[:, H:BANK], hT, I0, H),
-                (sum_og[:], hT, O0, 2 * H),
-            )
             for turned in range(2 * PASSES):
                 g, u = turned // 2, turned % 2
                 nc.tensor.transpose(
@@ -189,15 +186,31 @@ def tile_multiinputlstmcell_pa_kernel(
                     x_words[:, 256 * g + u : 256 * (g + 1) : 2],
                     ident_f32[:],
                 )
-            for out_cols, stateT, first, width in products:
-                for c in range(K_CHUNKS):
-                    nc.tensor.matmul(
-                        out_cols,
-                        lhsT=stateT[:, r, c, :],
-                        rhs=w_plain[:, c, first : first + width],
-                        start=(c == 0),
-                        stop=(c == K_CHUNKS - 1),
-                    )
+
+        def plain_product(out_cols, stateT, r, first, width):
+            for e in range(K_CHUNKS):
+                nc.tensor.matmul(
+                    out_cols,
+                    lhsT=stateT[:, r, :, e],
+                    rhs=w_plain[:, e, first : first + width],
+                    start=(e == 0),
+                    stop=(e == K_CHUNKS - 1),
+                )
+
+        def plain_a(r):
+            if r not in row_tiles:
+                return
+            sum_ai = psum.tile([P, BANK], F32, tag="bank")
+            sums[r] = [sum_ai]
+            plain_product(sum_ai[:, 0:H], cT, r, A0, H)
+
+        def plain_iog(r):
+            if r not in row_tiles:
+                return
+            sum_og = psum.tile([P, BANK], F32, tag="bank")
+            sums[r].append(sum_og)
+            plain_product(sums[r][0][:, H:BANK], hT, r, I0, H)
+            plain_product(sum_og[:], hT, r, O0, 2 * H)
 
         def x_out(r, half):
             if r not in row_tiles:
@@ -336,23 +349,35 @@ def tile_multiinputlstmcell_pa_kernel(
             )
             nc.sync.dma_start(out=h1_rows[:, r, :], in_=h_1[:])
 
-        for p in range(-LOOKAHEAD, ROW_TILES - 2):
+        turn_state(c_sb, cT, 0)
+        turn_state(h_sb, hT, 0)
+        plain_a(0)
+        spread_biases()
+        plain_iog(0)
+        plain_out(0, 0)
+        plain_out(0, 1)
+        for p in range(-X_AHEAD, ROW_TILES - 2):
             add_plain(p - 1, 1)
             subtract_a(p - 1)
             tanh_g(p - 1)
-            weave(p + LOOKAHEAD)
+            turn_x(p + X_AHEAD)
+            if p == 0:
+                turn_state(h_sb, hT, 1)
+                turn_state(c_sb, cT, 1)
+            plain_a(p + PLAIN_AHEAD)
+            plain_iog(p + PLAIN_AHEAD)
             mx_passes(p, 0)
-            quantise(p + LOOKAHEAD - 1)
+            quantise(p + X_AHEAD - 1)
             mx_passes(p, 1)
-            plain_out(p + LOOKAHEAD, 0)
+            plain_out(p + PLAIN_AHEAD, 0)
             summed_cell(p - 2)
-            plain_out(p + LOOKAHEAD, 1)
+            plain_out(p + PLAIN_AHEAD, 1)
             softmax_weight(p - 1)
             keep_weight(p - 1)
             new_hidden(p - 3)
-            x_out(p + LOOKAHEAD, 0)
+            x_out(p + X_AHEAD, 0)
             kept_cell(p - 1)
-            x_out(p + LOOKAHEAD, 1)
+            x_out(p + X_AHEAD, 1)
             add_plain(p, 0)
             sigmoid_ai(p)
             tanh_of_cell(p - 2)

@@ -67,8 +67,8 @@ def tile_multiinputlstmcell_pa_kernel(
         w_planes = keep.tile([P, PASSES, GATES], U8, align_bytes=64)
         x_codes = keep.tile([P, ROW_TILES, PASSES * P], U32, align_bytes=64)
         x_planes = keep.tile([P, ROW_TILES, PASSES * P], U8, align_bytes=64)
-        hT = keep.tile([P, ROW_TILES, P, K_CHUNKS], BF16)
-        cT = keep.tile([P, ROW_TILES, P, K_CHUNKS], BF16)
+        hT = keep.tile([P, ROW_TILES, K_CHUNKS, P], BF16)
+        cT = keep.tile([P, ROW_TILES, K_CHUNKS, P], BF16)
         ident_f32 = keep.tile([P, P], F32)
         ident_bf = keep.tile([P, P], BF16)
         ones = keep.tile([P, P], BF16)
@@ -118,11 +118,11 @@ def tile_multiinputlstmcell_pa_kernel(
 
         load_state(c_sb, c_rows, 0)
         nc.sync.dma_start(
-            out=w_plain[:, :, A0:I0], in_=alpha_weight_hh.rearrange("(p e) n -> p e n", e=K_CHUNKS)
+            out=w_plain[:, :, A0:I0], in_=alpha_weight_hh.rearrange("(c p) n -> p c n", p=P)
         )
         load_state(h_sb, h_rows, 0)
         nc.sync.dma_start(
-            out=w_plain[:, :, I0:GATES], in_=weight_hh.rearrange("(p e) n -> p e n", e=K_CHUNKS)
+            out=w_plain[:, :, I0:GATES], in_=weight_hh.rearrange("(c p) n -> p c n", p=P)
         )
         load_bias()
         load_x(0)
@@ -139,15 +139,16 @@ def tile_multiinputlstmcell_pa_kernel(
             load_x(r)
 
         def turn_state(state_sb, stateT, half):
-            words_ps = psum.tile([P, HALF, P], F32, tag="bank", name="words_ps")
-            for n in range(HALF):
-                nc.tensor.transpose(
-                    words_ps[:, n, :], state_sb[:, half * HALF + n, :].bitcast(F32), ident_f32[:]
-                )
-            tiles = slice(half * HALF, (half + 1) * HALF)
-            nc.vector.tensor_copy(
-                out=stateT[:, tiles, :, :].rearrange("p n r e -> p n (r e)").bitcast(F32), in_=words_ps[:]
-            )
+            for pair in range(half * HALF // 2, (half + 1) * HALF // 2):
+                st_ps = psum.tile([P, 2, K_CHUNKS, P], BF16, tag="bank", name="st_ps")
+                for n in range(2):
+                    for c in range(K_CHUNKS):
+                        nc.tensor.transpose(
+                            st_ps[:, n, c, :],
+                            state_sb[:, 2 * pair + n, c * P : (c + 1) * P],
+                            ident_bf[:],
+                        )
+                nc.vector.tensor_copy(out=stateT[:, 2 * pair : 2 * pair + 2, :, :], in_=st_ps[:])
 
         def spread_biases():
             for bank in range(GATES // BANK):
@@ -188,13 +189,13 @@ def tile_multiinputlstmcell_pa_kernel(
                 )
 
         def plain_product(out_cols, stateT, r, first, width):
-            for e in range(K_CHUNKS):
+            for c in range(K_CHUNKS):
                 nc.tensor.matmul(
                     out_cols,
-                    lhsT=stateT[:, r, :, e],
-                    rhs=w_plain[:, e, first : first + width],
-                    start=(e == 0),
-                    stop=(e == K_CHUNKS - 1),
+                    lhsT=stateT[:, r, c, :],
+                    rhs=w_plain[:, c, first : first + width],
+                    start=(c == 0),
+                    stop=(c == K_CHUNKS - 1),
                 )
 
         def plain_a(r):

@@ -23,8 +23,10 @@ GATES = 4 * H
 BANK = 512
 A0, I0, O0, G0 = 0, H, 2 * H, 3 * H
 X_AHEAD = 2
-PLAIN_AHEAD = 3
+PLAIN_AHEAD = 4
 HALF = ROW_TILES // 2
+ALL = slice(0, H)
+LEFT, RIGHT = slice(0, H // 2), slice(H // 2, H)
 
 FLOPS = 2 * B * I * GATES + 2 * B * H * GATES
 
@@ -113,8 +115,8 @@ def tile_multiinputlstmcell_pa_kernel(
             nc.sync.dma_start(out=state_sb[:, tiles, :], in_=rows_view[:, tiles, :])
 
         def load_bias():
-            nc.sync.dma_start(out=bias_rows[0:1, A0:I0], in_=alpha_bias.unsqueeze(0))
-            nc.sync.dma_start(out=bias_rows[0:1, I0:GATES], in_=bias.unsqueeze(0))
+            nc.gpsimd.dma_start(out=bias_rows[0:1, A0:I0], in_=alpha_bias.unsqueeze(0))
+            nc.gpsimd.dma_start(out=bias_rows[0:1, I0:GATES], in_=bias.unsqueeze(0))
 
         load_state(c_sb, c_rows, 0)
         nc.sync.dma_start(
@@ -126,15 +128,15 @@ def tile_multiinputlstmcell_pa_kernel(
         )
         load_bias()
         load_x(0)
+        load_state(h_sb, h_rows, 1)
         load_scales(0)
+        load_state(c_sb, c_rows, 1)
         load_x(1)
         load_scales(1)
-        load_x(2)
-        load_scales(2)
-        load_state(h_sb, h_rows, 1)
-        load_scales(3)
         load_words()
-        load_state(c_sb, c_rows, 1)
+        load_scales(2)
+        load_x(2)
+        load_scales(3)
         for r in range(3, ROW_TILES):
             load_x(r)
 
@@ -172,6 +174,7 @@ def tile_multiinputlstmcell_pa_kernel(
         step = {}
         c_1 = {}
         tanh_c = {}
+        h_1 = {}
 
         def turn_x(r):
             if r not in row_tiles:
@@ -258,97 +261,111 @@ def tile_multiinputlstmcell_pa_kernel(
                     stop=(g == PASSES - 1),
                 )
 
-        def add_plain(r, bank):
+        def tile_of(store, r, cols, name, pool=work, width=H):
+            if cols.start == 0:
+                store[r] = pool.tile([P, width], F32, name=name)
+            return store[r]
+
+        def both(ap, cols):
+            return ap.rearrange("p (gate n) -> p gate n", gate=2)[:, :, cols]
+
+        def add_ai(r, cols=ALL):
             if r not in row_tiles:
                 return
-            if bank == 0:
-                pre[r] = work.tile([P, GATES], F32, name="pre")
-            cols = slice(bank * BANK, (bank + 1) * BANK)
+            out = tile_of(pre, r, cols, "pre", width=GATES)
             nc.vector.tensor_tensor(
-                out=pre[r][:, cols], in0=acc[(r, bank)][:], in1=plain_sb[r][:, cols], op=ALU.add
+                out=both(out[:, A0:O0], cols),
+                in0=both(acc[(r, 0)][:], cols),
+                in1=both(plain_sb[r][:, A0:O0], cols),
+                op=ALU.add,
             )
 
-        def add_plain_gate(r, first):
-            cols = slice(first, first + H)
+        def add_og(r, first=O0, width=2 * H):
+            if r not in row_tiles:
+                return
+            cols = slice(first, first + width)
             nc.vector.tensor_tensor(
                 out=pre[r][:, cols],
-                in0=acc[(r, 1)][:, first - BANK : first - BANK + H],
+                in0=acc[(r, 1)][:, first - BANK : first - BANK + width],
                 in1=plain_sb[r][:, cols],
                 op=ALU.add,
             )
 
-        def sigmoid_ai(r):
+        def sigmoid_ai(r, cols=ALL):
             if r not in row_tiles:
                 return
-            gates[r] = long_lived.tile([P, GATES], F32, name="gates")
-            nc.scalar.activation(out=gates[r][:, A0:O0], in_=pre[r][:, A0:O0], func=ACT.Sigmoid)
+            out = tile_of(gates, r, cols, "gates", long_lived, GATES)
+            nc.scalar.activation(
+                out=both(out[:, A0:O0], cols), in_=both(pre[r][:, A0:O0], cols), func=ACT.Sigmoid
+            )
 
-        def tanh_g(r):
+        def gate(first, cols):
+            return slice(first + cols.start, first + cols.stop)
+
+        def tanh_g(r, cols=ALL):
             if r not in row_tiles:
                 return
-            nc.scalar.activation(out=gates[r][:, G0:GATES], in_=pre[r][:, G0:GATES], func=ACT.Tanh)
+            g = gate(G0, cols)
+            nc.scalar.activation(out=gates[r][:, g], in_=pre[r][:, g], func=ACT.Tanh)
 
         def sigmoid_o(r):
             if r not in row_tiles:
                 return
             nc.scalar.activation(out=gates[r][:, O0:G0], in_=pre[r][:, O0:G0], func=ACT.Sigmoid)
 
-        def subtracter(r):
-            return nc.vector if r == ROW_TILES - 1 else nc.gpsimd
-
-        def subtract_a(r, engine=None):
+        def subtract_a(r, cols=ALL, engine=nc.gpsimd):
             if r not in row_tiles:
                 return
-            i_minus_a[r] = work.tile([P, H], F32, name="i_minus_a")
-            (engine or subtracter(r)).tensor_tensor(
-                out=i_minus_a[r][:], in0=gates[r][:, I0:O0], in1=gates[r][:, A0:I0], op=ALU.subtract
+            out = tile_of(i_minus_a, r, cols, "i_minus_a")
+            engine.tensor_tensor(
+                out=out[:, cols], in0=gates[r][:, gate(I0, cols)], in1=gates[r][:, gate(A0, cols)], op=ALU.subtract
             )
 
-        def softmax_weight(r):
+        def softmax_weight(r, cols=ALL):
             if r not in row_tiles:
                 return
-            w_i[r] = work.tile([P, H], F32, name="w_i")
-            nc.scalar.activation(out=w_i[r][:], in_=i_minus_a[r][:], func=ACT.Sigmoid)
+            out = tile_of(w_i, r, cols, "w_i")
+            nc.scalar.activation(out=out[:, cols], in_=i_minus_a[r][:, cols], func=ACT.Sigmoid)
 
-        def keep_weight(r):
+        def keep_weight(r, cols=ALL):
             if r not in row_tiles:
                 return
-            w_a[r] = work.tile([P, H], F32, name="w_a")
-            nc.scalar.activation(out=w_a[r][:], in_=i_minus_a[r][:], func=ACT.Sigmoid, scale=-1.0)
+            out = tile_of(w_a, r, cols, "w_a")
+            nc.scalar.activation(out=out[:, cols], in_=i_minus_a[r][:, cols], func=ACT.Sigmoid, scale=-1.0)
 
-        def kept_cell(r, engine=None):
+        def kept_cell(r, cols=ALL, engine=nc.gpsimd):
             if r not in row_tiles:
                 return
-            kept[r] = work.tile([P, H], F32, name="kept")
-            (engine or subtracter(r)).tensor_tensor(out=kept[r][:], in0=w_a[r][:], in1=c_sb[:, r, :], op=ALU.mult)
+            out = tile_of(kept, r, cols, "kept")
+            engine.tensor_tensor(out=out[:, cols], in0=w_a[r][:, cols], in1=c_sb[:, r, cols], op=ALU.mult)
 
-        def new_part(r):
+        def new_part(r, cols=ALL):
             if r not in row_tiles:
                 return
-            step[r] = work.tile([P, H], F32, name="step")
-            nc.vector.tensor_tensor(out=step[r][:], in0=w_i[r][:], in1=gates[r][:, G0:GATES], op=ALU.mult)
+            out = tile_of(step, r, cols, "step")
+            nc.vector.tensor_tensor(out=out[:, cols], in0=w_i[r][:, cols], in1=gates[r][:, gate(G0, cols)], op=ALU.mult)
 
-        def summed_cell(r):
+        def summed_cell(r, cols=ALL):
             if r not in row_tiles:
                 return
-            c_1[r] = work.tile([P, H], F32, name="c_1")
-            nc.vector.tensor_tensor(out=c_1[r][:], in0=step[r][:], in1=kept[r][:], op=ALU.add)
-            nc.sync.dma_start(out=c1_rows[:, r, :], in_=c_1[r][:])
+            out = tile_of(c_1, r, cols, "c_1")
+            nc.vector.tensor_tensor(out=out[:, cols], in0=step[r][:, cols], in1=kept[r][:, cols], op=ALU.add)
+            nc.sync.dma_start(out=c1_rows[:, r, cols], in_=out[:, cols])
 
-        def tanh_of_cell(r):
+        def tanh_of_cell(r, cols=ALL):
             if r not in row_tiles:
                 return
-            tanh_c[r] = work.tile([P, H], F32, name="tanh_c")
-            nc.scalar.activation(out=tanh_c[r][:], in_=c_1[r][:], func=ACT.Tanh)
+            out = tile_of(tanh_c, r, cols, "tanh_c")
+            nc.scalar.activation(out=out[:, cols], in_=c_1[r][:, cols], func=ACT.Tanh)
 
-        def new_hidden(r, engine=None):
+        def new_hidden(r, cols=ALL, engine=nc.gpsimd):
             if r not in row_tiles:
                 return
-            h_1 = work.tile([P, H], F32, name="h_1")
-            (engine or nc.gpsimd).tensor_tensor(
-                out=h_1[:], in0=gates[r][:, O0:G0], in1=tanh_c[r][:], op=ALU.mult
+            out = tile_of(h_1, r, cols, "h_1")
+            engine.tensor_tensor(
+                out=out[:, cols], in0=gates[r][:, gate(O0, cols)], in1=tanh_c[r][:, cols], op=ALU.mult
             )
-            nc.sync.dma_start(out=h1_rows[:, r, :], in_=h_1[:])
+            nc.sync.dma_start(out=h1_rows[:, r, cols], in_=out[:, cols])
 
         turn_state(c_sb, cT, 0)
         turn_state(h_sb, hT, 0)
@@ -357,80 +374,84 @@ def tile_multiinputlstmcell_pa_kernel(
         plain_iog(0)
         plain_out(0, 0)
         plain_out(0, 1)
-        for p in range(-X_AHEAD, ROW_TILES - 2):
-            add_plain(p - 1, 1)
-            subtract_a(p - 1)
-            tanh_g(p - 1)
-            turn_x(p + X_AHEAD)
-            if p == 0:
+        plain_a(1)
+        plain_iog(1)
+        plain_out(1, 0)
+        plain_out(1, 1)
+        for p in range(-1, ROW_TILES - 1):
+            turn_x(p + 1)
+            if p == -1:
+                plain_a(2)
+                plain_iog(2)
+                x_out(0, 0)
+                x_out(0, 1)
+                plain_out(2, 0)
+                plain_out(2, 1)
+                quantise(0)
                 turn_state(h_sb, hT, 1)
                 turn_state(c_sb, cT, 1)
             plain_a(p + PLAIN_AHEAD)
             plain_iog(p + PLAIN_AHEAD)
-            mx_passes(p, 0)
-            quantise(p + X_AHEAD - 1)
-            mx_passes(p, 1)
-            plain_out(p + PLAIN_AHEAD, 0)
+            add_og(p - 1)
+            subtract_a(p - 1)
             summed_cell(p - 2)
-            plain_out(p + PLAIN_AHEAD, 1)
+            if p >= 0:
+                x_out(p + 1, 0)
+                x_out(p + 1, 1)
             softmax_weight(p - 1)
             keep_weight(p - 1)
-            new_hidden(p - 3)
-            x_out(p + X_AHEAD, 0)
+            tanh_g(p - 1)
+            plain_out(p + PLAIN_AHEAD, 0)
+            if p >= 0:
+                quantise(p + 1)
             kept_cell(p - 1)
-            x_out(p + X_AHEAD, 1)
-            add_plain(p, 0)
-            sigmoid_ai(p)
+            plain_out(p + PLAIN_AHEAD, 1)
+            mx_passes(p, 0)
+            mx_passes(p, 1)
             tanh_of_cell(p - 2)
-            new_part(p - 1)
             sigmoid_o(p - 1)
-
-
-        quantise(7)
-        add_plain(5, 1)
-        subtract_a(5)
-        tanh_g(5)
-        mx_passes(6, 0)
+            new_hidden(p - 2)
+            add_ai(p)
+            new_part(p - 1)
+            sigmoid_ai(p)
         mx_passes(7, 0)
-        mx_passes(6, 1)
         mx_passes(7, 1)
-        summed_cell(4)
-        softmax_weight(5)
-        keep_weight(5)
-        new_hidden(3)
-        kept_cell(5)
-        add_plain(6, 0)
-        sigmoid_ai(6)
-        tanh_of_cell(4)
-        new_part(5)
-        add_plain(7, 0)
-        sigmoid_ai(7)
-        new_hidden(4)
-        subtract_a(6, nc.vector)
+        subtract_a(6, engine=nc.vector)
+        add_og(6)
         softmax_weight(6)
-        sigmoid_o(5)
-        add_plain_gate(6, G0)
-        tanh_g(6)
         keep_weight(6)
+        tanh_g(6)
         summed_cell(5)
-        add_plain_gate(6, O0)
-        subtract_a(7, nc.vector)
-        softmax_weight(7)
-        keep_weight(7)
-        tanh_of_cell(5)
+        kept_cell(6)
+        add_ai(7, LEFT)
+        sigmoid_ai(7, LEFT)
+        add_ai(7, RIGHT)
+        sigmoid_ai(7, RIGHT)
+        subtract_a(7, LEFT, nc.vector)
         new_part(6)
-        kept_cell(6, nc.vector)
-        add_plain_gate(7, G0)
-        tanh_g(7)
-        sigmoid_o(6)
+        tanh_of_cell(5)
+        softmax_weight(7, LEFT)
+        subtract_a(7, RIGHT, nc.vector)
+        keep_weight(7, LEFT)
+        softmax_weight(7, RIGHT)
+        keep_weight(7, RIGHT)
         summed_cell(6)
-        kept_cell(7, nc.vector)
-        new_hidden(5)
+        add_og(7, G0, H)
+        tanh_g(7, LEFT)
+        tanh_g(7, RIGHT)
+        add_og(7, O0, H)
+        kept_cell(7, LEFT, nc.vector)
+        kept_cell(7, RIGHT, nc.vector)
+        sigmoid_o(6)
         tanh_of_cell(6)
-        new_part(7)
-        add_plain_gate(7, O0)
-        summed_cell(7)
+        new_part(7, LEFT)
+        summed_cell(7, LEFT)
+        new_part(7, RIGHT)
+        summed_cell(7, RIGHT)
         sigmoid_o(7)
-        tanh_of_cell(7)
-        new_hidden(6, nc.vector)
-        new_hidden(7, nc.vector)
+        tanh_of_cell(7, LEFT)
+        tanh_of_cell(7, RIGHT)
+        new_hidden(5)
+        new_hidden(6, engine=nc.vector)
+        new_hidden(7, LEFT, nc.vector)
+        new_hidden(7, RIGHT, nc.vector)

@@ -74,11 +74,13 @@ def tile_multiinputlstmcell_pa_kernel(
         ident_f32 = keep.tile([P, P], F32)
         ident_bf = keep.tile([P, P], BF16)
         ones = keep.tile([P, P], BF16)
+        zeros = keep.tile([P, BANK], BF16)
         bias_rows = keep.tile([P, GATES], BF16)
         bias_all = keep.tile([P, GATES], F32)
         table_in = keep.tile([P, 1], F32)
         table_out = keep.tile([P, 1], F32)
 
+        nc.gpsimd.memset(zeros[:], 0.0)
         nc.vector.memset(w_planes[:].bitcast(I32), 0)
         nc.vector.memset(bias_rows[:], 0.0)
         nc.vector.memset(ones[:], 1.0)
@@ -115,8 +117,8 @@ def tile_multiinputlstmcell_pa_kernel(
             nc.sync.dma_start(out=state_sb[:, tiles, :], in_=rows_view[:, tiles, :])
 
         def load_bias():
-            nc.gpsimd.dma_start(out=bias_rows[0:1, A0:I0], in_=alpha_bias.unsqueeze(0))
-            nc.gpsimd.dma_start(out=bias_rows[0:1, I0:GATES], in_=bias.unsqueeze(0))
+            nc.sync.dma_start(out=bias_rows[0:1, A0:I0], in_=alpha_bias.unsqueeze(0))
+            nc.sync.dma_start(out=bias_rows[0:1, I0:GATES], in_=bias.unsqueeze(0))
 
         load_state(c_sb, c_rows, 0)
         nc.sync.dma_start(
@@ -140,17 +142,21 @@ def tile_multiinputlstmcell_pa_kernel(
         for r in range(3, ROW_TILES):
             load_x(r)
 
-        def turn_state(state_sb, stateT, half):
-            for pair in range(half * HALF // 2, (half + 1) * HALF // 2):
-                st_ps = psum.tile([P, 2, K_CHUNKS, P], BF16, tag="bank", name="st_ps")
-                for n in range(2):
-                    for c in range(K_CHUNKS):
-                        nc.tensor.transpose(
-                            st_ps[:, n, c, :],
-                            state_sb[:, 2 * pair + n, c * P : (c + 1) * P],
-                            ident_bf[:],
-                        )
-                nc.vector.tensor_copy(out=stateT[:, 2 * pair : 2 * pair + 2, :, :], in_=st_ps[:])
+        def turn_state(state_sb, stateT, pair):
+            st_ps = psum.tile([P, 2, K_CHUNKS, P], BF16, tag="bank", name="st_ps")
+            for n in range(2):
+                for c in range(K_CHUNKS):
+                    nc.tensor.transpose(
+                        st_ps[:, n, c, :],
+                        state_sb[:, 2 * pair + n, c * P : (c + 1) * P],
+                        ident_bf[:],
+                    )
+            nc.vector.tensor_copy(out=stateT[:, 2 * pair : 2 * pair + 2, :, :], in_=st_ps[:])
+
+        def keep_awake(count):
+            idle_ps = psum.tile([P, BANK], F32, tag="bank", name="idle_ps")
+            for unused in range(count):
+                nc.tensor.matmul(idle_ps[:], lhsT=zeros[:, 0:P], rhs=zeros[:], start=True, stop=True)
 
         def spread_biases():
             for bank in range(GATES // BANK):
@@ -339,6 +345,25 @@ def tile_multiinputlstmcell_pa_kernel(
             out = tile_of(kept, r, cols, "kept")
             engine.tensor_tensor(out=out[:, cols], in0=w_a[r][:, cols], in1=c_sb[:, r, cols], op=ALU.mult)
 
+        def new_minus_old(r, engine=nc.gpsimd):
+            if r not in row_tiles:
+                return
+            out = tile_of(kept, r, ALL, "kept")
+            engine.tensor_tensor(out=out[:], in0=gates[r][:, G0:GATES], in1=c_sb[:, r, :], op=ALU.subtract)
+
+        def scaled_step(r):
+            if r not in row_tiles:
+                return
+            out = tile_of(step, r, ALL, "step")
+            nc.vector.tensor_tensor(out=out[:], in0=w_i[r][:], in1=kept[r][:], op=ALU.mult)
+
+        def stepped_cell(r):
+            if r not in row_tiles:
+                return
+            out = tile_of(c_1, r, ALL, "c_1")
+            nc.vector.tensor_tensor(out=out[:], in0=step[r][:], in1=c_sb[:, r, :], op=ALU.add)
+            nc.sync.dma_start(out=c1_rows[:, r, :], in_=out[:])
+
         def new_part(r, cols=ALL):
             if r not in row_tiles:
                 return
@@ -367,8 +392,12 @@ def tile_multiinputlstmcell_pa_kernel(
             )
             nc.sync.dma_start(out=h1_rows[:, r, cols], in_=out[:, cols])
 
+        keep_awake(4)
         turn_state(c_sb, cT, 0)
+        turn_state(c_sb, cT, 1)
+        keep_awake(1)
         turn_state(h_sb, hT, 0)
+        turn_state(h_sb, hT, 1)
         plain_a(0)
         spread_biases()
         plain_iog(0)
@@ -378,80 +407,95 @@ def tile_multiinputlstmcell_pa_kernel(
         plain_iog(1)
         plain_out(1, 0)
         plain_out(1, 1)
-        for p in range(-1, ROW_TILES - 1):
+        turn_x(0)
+        x_out(0, 0)
+        x_out(0, 1)
+        plain_a(2)
+        plain_iog(2)
+        plain_out(2, 0)
+        quantise(0)
+        plain_out(2, 1)
+        turn_state(h_sb, hT, 2)
+        turn_state(c_sb, cT, 2)
+        plain_a(3)
+        plain_iog(3)
+        plain_out(3, 0)
+        plain_out(3, 1)
+        for p in range(0, ROW_TILES - 2):
             turn_x(p + 1)
-            if p == -1:
-                plain_a(2)
-                plain_iog(2)
-                x_out(0, 0)
-                x_out(0, 1)
-                plain_out(2, 0)
-                plain_out(2, 1)
-                quantise(0)
-                turn_state(h_sb, hT, 1)
-                turn_state(c_sb, cT, 1)
+            if p == ROW_TILES - 3:
+                turn_x(p + 2)
             plain_a(p + PLAIN_AHEAD)
             plain_iog(p + PLAIN_AHEAD)
             add_og(p - 1)
             subtract_a(p - 1)
-            summed_cell(p - 2)
-            if p >= 0:
-                x_out(p + 1, 0)
-                x_out(p + 1, 1)
-            softmax_weight(p - 1)
-            keep_weight(p - 1)
+            stepped_cell(p - 2)
+            x_out(p + 1, 0)
+            x_out(p + 1, 1)
             tanh_g(p - 1)
+            new_minus_old(p - 1)
+            if p == ROW_TILES - 3:
+                x_out(p + 2, 0)
+                x_out(p + 2, 1)
+            softmax_weight(p - 1)
             plain_out(p + PLAIN_AHEAD, 0)
-            if p >= 0:
-                quantise(p + 1)
-            kept_cell(p - 1)
+            quantise(p + 1)
             plain_out(p + PLAIN_AHEAD, 1)
+            if p == 0:
+                turn_state(h_sb, hT, 3)
+                turn_state(c_sb, cT, 3)
             mx_passes(p, 0)
             mx_passes(p, 1)
             tanh_of_cell(p - 2)
             sigmoid_o(p - 1)
             new_hidden(p - 2)
             add_ai(p)
-            new_part(p - 1)
+            if p == ROW_TILES - 3:
+                quantise(p + 2)
+            scaled_step(p - 1)
             sigmoid_ai(p)
+        add_og(5)
+        subtract_a(5)
+        tanh_g(5)
+        mx_passes(6, 0)
         mx_passes(7, 0)
+        mx_passes(6, 1)
         mx_passes(7, 1)
+        add_ai(6)
+        new_minus_old(5)
+        sigmoid_ai(6)
+        softmax_weight(5)
+        sigmoid_o(5)
+        add_ai(7)
+        stepped_cell(4)
+        tanh_of_cell(4)
+        scaled_step(5)
+        sigmoid_ai(7)
         subtract_a(6, engine=nc.vector)
-        add_og(6)
-        softmax_weight(6)
-        keep_weight(6)
-        tanh_g(6)
-        summed_cell(5)
-        kept_cell(6)
-        add_ai(7, LEFT)
-        sigmoid_ai(7, LEFT)
-        add_ai(7, RIGHT)
-        sigmoid_ai(7, RIGHT)
-        subtract_a(7, LEFT, nc.vector)
-        new_part(6)
+        stepped_cell(5)
         tanh_of_cell(5)
-        softmax_weight(7, LEFT)
-        subtract_a(7, RIGHT, nc.vector)
-        keep_weight(7, LEFT)
-        softmax_weight(7, RIGHT)
-        keep_weight(7, RIGHT)
-        summed_cell(6)
+        new_hidden(4)
+        keep_weight(6)
+        softmax_weight(6)
+        add_og(6, G0, H)
         add_og(7, G0, H)
-        tanh_g(7, LEFT)
-        tanh_g(7, RIGHT)
+        subtract_a(7, engine=nc.vector)
+        keep_weight(7)
+        tanh_g(6)
+        tanh_g(7)
+        softmax_weight(7)
+        add_og(6, O0, H)
         add_og(7, O0, H)
-        kept_cell(7, LEFT, nc.vector)
-        kept_cell(7, RIGHT, nc.vector)
-        sigmoid_o(6)
-        tanh_of_cell(6)
-        new_part(7, LEFT)
-        summed_cell(7, LEFT)
-        new_part(7, RIGHT)
-        summed_cell(7, RIGHT)
-        sigmoid_o(7)
-        tanh_of_cell(7, LEFT)
-        tanh_of_cell(7, RIGHT)
         new_hidden(5)
+        kept_cell(6, engine=nc.vector)
+        kept_cell(7, engine=nc.vector)
+        new_part(6)
+        new_part(7)
+        summed_cell(6)
+        summed_cell(7)
+        sigmoid_o(6)
+        sigmoid_o(7)
+        tanh_of_cell(6)
+        tanh_of_cell(7)
         new_hidden(6, engine=nc.vector)
-        new_hidden(7, LEFT, nc.vector)
-        new_hidden(7, RIGHT, nc.vector)
+        new_hidden(7, engine=nc.vector)

@@ -102,11 +102,13 @@ def tile_multiinputlstmcell_pa_kernel(
                 in_=weight_ih_scales[:, j:16:4, :].rearrange("g q n -> q g n").bitcast(I32),
             )
 
-        def load_words():
+        def load_alpha_words():
             nc.sync.dma_start(
                 out=w_words[:, :, 2 * A0 : 2 * I0].bitcast(I32),
                 in_=alpha_weight_ih_words.rearrange("g p b -> p g b").bitcast(I32),
             )
+
+        def load_gate_words():
             nc.sync.dma_start(
                 out=w_words[:, :, 2 * I0 : 2 * GATES].bitcast(I32),
                 in_=weight_ih_words.rearrange("g p b -> p g b").bitcast(I32),
@@ -130,15 +132,16 @@ def tile_multiinputlstmcell_pa_kernel(
         )
         load_bias()
         load_x(0)
-        load_state(h_sb, h_rows, 1)
         load_scales(0)
+        load_state(h_sb, h_rows, 1)
         load_state(c_sb, c_rows, 1)
-        load_x(1)
         load_scales(1)
-        load_words()
+        load_x(1)
+        load_alpha_words()
         load_scales(2)
-        load_x(2)
+        load_gate_words()
         load_scales(3)
+        load_x(2)
         for r in range(3, ROW_TILES):
             load_x(r)
 

@@ -81,8 +81,8 @@ def tile_multiinputlstmcell_pa_kernel(
         table_out = keep.tile([P, 1], F32)
 
         nc.gpsimd.memset(zeros[:], 0.0)
-        nc.vector.memset(w_planes[:].bitcast(I32), 0)
         nc.vector.memset(bias_rows[:], 0.0)
+        nc.vector.memset(w_planes[:].bitcast(I32), 0)
         nc.vector.memset(ones[:], 1.0)
         nc.vector.memset(table_in[:], 0.0)
         nc.scalar.activation(out=table_out[:], in_=table_in[:], func=ACT.Sigmoid)
@@ -114,8 +114,8 @@ def tile_multiinputlstmcell_pa_kernel(
                 in_=weight_ih_words.rearrange("g p b -> p g b").bitcast(I32),
             )
 
-        def load_state(state_sb, rows_view, half):
-            tiles = slice(half * HALF, (half + 1) * HALF)
+        def load_state(state_sb, rows_view, pair):
+            tiles = slice(2 * pair, 2 * pair + 2)
             nc.sync.dma_start(out=state_sb[:, tiles, :], in_=rows_view[:, tiles, :])
 
         def load_bias():
@@ -127,14 +127,16 @@ def tile_multiinputlstmcell_pa_kernel(
             out=w_plain[:, :, A0:I0], in_=alpha_weight_hh.rearrange("(c p) n -> p c n", p=P)
         )
         load_state(h_sb, h_rows, 0)
+        load_bias()
         nc.sync.dma_start(
             out=w_plain[:, :, I0:GATES], in_=weight_hh.rearrange("(c p) n -> p c n", p=P)
         )
-        load_bias()
+        load_state(c_sb, c_rows, 1)
+        load_state(h_sb, h_rows, 1)
         load_x(0)
         load_scales(0)
-        load_state(h_sb, h_rows, 1)
-        load_state(c_sb, c_rows, 1)
+        load_state(c_sb, c_rows, 2)
+        load_state(h_sb, h_rows, 2)
         load_scales(1)
         load_x(1)
         load_alpha_words()
@@ -142,6 +144,8 @@ def tile_multiinputlstmcell_pa_kernel(
         load_gate_words()
         load_scales(3)
         load_x(2)
+        load_state(c_sb, c_rows, 3)
+        load_state(h_sb, h_rows, 3)
         for r in range(3, ROW_TILES):
             load_x(r)
 
@@ -166,7 +170,7 @@ def tile_multiinputlstmcell_pa_kernel(
                 cols = slice(bank * BANK, (bank + 1) * BANK)
                 bias_ps = psum.tile([P, BANK], F32, tag="bank", name="bias_ps")
                 nc.tensor.matmul(bias_ps[:], lhsT=ones[:], rhs=bias_rows[:, cols], start=True, stop=True)
-                nc.vector.tensor_copy(out=bias_all[:, cols], in_=bias_ps[:])
+                nc.scalar.copy(out=bias_all[:, cols], in_=bias_ps[:])
 
         row_tiles = range(ROW_TILES)
         xt = {}
@@ -397,29 +401,29 @@ def tile_multiinputlstmcell_pa_kernel(
 
         keep_awake(4)
         turn_state(c_sb, cT, 0)
-        turn_state(c_sb, cT, 1)
         keep_awake(1)
         turn_state(h_sb, hT, 0)
-        turn_state(h_sb, hT, 1)
         plain_a(0)
         spread_biases()
         plain_iog(0)
         plain_out(0, 0)
         plain_out(0, 1)
+        turn_state(c_sb, cT, 1)
+        turn_state(h_sb, hT, 1)
         plain_a(1)
         plain_iog(1)
         plain_out(1, 0)
-        plain_out(1, 1)
         turn_x(0)
         x_out(0, 0)
         x_out(0, 1)
+        plain_out(1, 1)
         plain_a(2)
         plain_iog(2)
         plain_out(2, 0)
         quantise(0)
-        plain_out(2, 1)
-        turn_state(h_sb, hT, 2)
         turn_state(c_sb, cT, 2)
+        turn_state(h_sb, hT, 2)
+        plain_out(2, 1)
         plain_a(3)
         plain_iog(3)
         plain_out(3, 0)
@@ -444,9 +448,9 @@ def tile_multiinputlstmcell_pa_kernel(
             plain_out(p + PLAIN_AHEAD, 0)
             quantise(p + 1)
             plain_out(p + PLAIN_AHEAD, 1)
-            if p == 0:
-                turn_state(h_sb, hT, 3)
+            if p == 1:
                 turn_state(c_sb, cT, 3)
+                turn_state(h_sb, hT, 3)
             mx_passes(p, 0)
             mx_passes(p, 1)
             tanh_of_cell(p - 2)

@@ -23,7 +23,7 @@ GATES = 4 * H
 BANK = 512
 A0, I0, O0, G0 = 0, H, 2 * H, 3 * H
 X_AHEAD = 2
-PLAIN_AHEAD = 4
+PLAIN_BEFORE = {0: (4, 5), 1: (6,), 2: (7,)}
 HALF = ROW_TILES // 2
 ALL = slice(0, H)
 LEFT, RIGHT = slice(0, H // 2), slice(H // 2, H)
@@ -51,7 +51,7 @@ def tile_multiinputlstmcell_pa_kernel(
     with ExitStack() as ctx:
         keep = ctx.enter_context(tc.tile_pool(name="keep", bufs=1))
         work = ctx.enter_context(tc.tile_pool(name="work", bufs=3))
-        long_lived = ctx.enter_context(tc.tile_pool(name="long_lived", bufs=PLAIN_AHEAD + 2))
+        long_lived = ctx.enter_context(tc.tile_pool(name="long_lived", bufs=ROW_TILES))
         psum = ctx.enter_context(tc.psum_pool(name="psum", bufs=8))
         ctx.enter_context(tc.manual_schedule())
 
@@ -143,10 +143,9 @@ def tile_multiinputlstmcell_pa_kernel(
         load_scales(2)
         load_gate_words()
         load_scales(3)
-        load_x(2)
         load_state(c_sb, c_rows, 3)
         load_state(h_sb, h_rows, 3)
-        for r in range(3, ROW_TILES):
+        for r in range(2, ROW_TILES):
             load_x(r)
 
         def turn_state(state_sb, stateT, pair):
@@ -429,12 +428,17 @@ def tile_multiinputlstmcell_pa_kernel(
         plain_out(3, 0)
         plain_out(3, 1)
         for p in range(0, ROW_TILES - 2):
+            plain = PLAIN_BEFORE.get(p, ())
+            add_og(p - 1)
+            if p == 1:
+                turn_state(c_sb, cT, 3)
+                turn_state(h_sb, hT, 3)
             turn_x(p + 1)
             if p == ROW_TILES - 3:
                 turn_x(p + 2)
-            plain_a(p + PLAIN_AHEAD)
-            plain_iog(p + PLAIN_AHEAD)
-            add_og(p - 1)
+            for r in plain:
+                plain_a(r)
+                plain_iog(r)
             subtract_a(p - 1)
             stepped_cell(p - 2)
             x_out(p + 1, 0)
@@ -445,12 +449,14 @@ def tile_multiinputlstmcell_pa_kernel(
                 x_out(p + 2, 0)
                 x_out(p + 2, 1)
             softmax_weight(p - 1)
-            plain_out(p + PLAIN_AHEAD, 0)
+            for r in plain[:1]:
+                plain_out(r, 0)
             quantise(p + 1)
-            plain_out(p + PLAIN_AHEAD, 1)
-            if p == 1:
-                turn_state(c_sb, cT, 3)
-                turn_state(h_sb, hT, 3)
+            for r in plain[:1]:
+                plain_out(r, 1)
+            for r in plain[1:]:
+                plain_out(r, 0)
+                plain_out(r, 1)
             mx_passes(p, 0)
             mx_passes(p, 1)
             tanh_of_cell(p - 2)

@@ -74,14 +74,14 @@ def tile_multiinputlstmcell_pa_kernel(
         ident_f32 = keep.tile([P, P], F32)
         ident_bf = keep.tile([P, P], BF16)
         ones = keep.tile([P, P], BF16)
-        zeros = keep.tile([P, BANK], BF16)
+        zeros = keep.tile([P, P], BF16)
         bias_rows = keep.tile([P, GATES], BF16)
         bias_all = keep.tile([P, GATES], F32)
         table_in = keep.tile([P, 1], F32)
         table_out = keep.tile([P, 1], F32)
 
-        nc.gpsimd.memset(zeros[:], 0.0)
-        nc.vector.memset(bias_rows[:], 0.0)
+        nc.vector.memset(zeros[:].bitcast(I32), 0)
+        nc.vector.memset(bias_rows[:].bitcast(I32), 0)
         nc.vector.memset(w_planes[:].bitcast(I32), 0)
         nc.vector.memset(ones[:], 1.0)
         nc.vector.memset(table_in[:], 0.0)
@@ -139,12 +139,12 @@ def tile_multiinputlstmcell_pa_kernel(
         load_state(h_sb, h_rows, 2)
         load_scales(1)
         load_x(1)
+        load_state(c_sb, c_rows, 3)
+        load_state(h_sb, h_rows, 3)
         load_alpha_words()
         load_scales(2)
         load_gate_words()
         load_scales(3)
-        load_state(c_sb, c_rows, 3)
-        load_state(h_sb, h_rows, 3)
         for r in range(2, ROW_TILES):
             load_x(r)
 
@@ -162,7 +162,7 @@ def tile_multiinputlstmcell_pa_kernel(
         def keep_awake(count):
             idle_ps = psum.tile([P, BANK], F32, tag="bank", name="idle_ps")
             for unused in range(count):
-                nc.tensor.matmul(idle_ps[:], lhsT=zeros[:, 0:P], rhs=zeros[:], start=True, stop=True)
+                nc.tensor.matmul(idle_ps[:, 0:P], lhsT=zeros[:], rhs=zeros[:], start=True, stop=True)
 
         def spread_biases():
             for bank in range(GATES // BANK):
@@ -398,12 +398,12 @@ def tile_multiinputlstmcell_pa_kernel(
             )
             nc.sync.dma_start(out=h1_rows[:, r, cols], in_=out[:, cols])
 
-        keep_awake(4)
+        keep_awake(14)
         turn_state(c_sb, cT, 0)
-        keep_awake(1)
+        keep_awake(4)
         turn_state(h_sb, hT, 0)
-        plain_a(0)
         spread_biases()
+        plain_a(0)
         plain_iog(0)
         plain_out(0, 0)
         plain_out(0, 1)
@@ -429,16 +429,16 @@ def tile_multiinputlstmcell_pa_kernel(
         plain_out(3, 1)
         for p in range(0, ROW_TILES - 2):
             plain = PLAIN_BEFORE.get(p, ())
-            add_og(p - 1)
-            if p == 1:
-                turn_state(c_sb, cT, 3)
-                turn_state(h_sb, hT, 3)
             turn_x(p + 1)
             if p == ROW_TILES - 3:
                 turn_x(p + 2)
             for r in plain:
                 plain_a(r)
                 plain_iog(r)
+                if r == 4:
+                    turn_state(c_sb, cT, 3)
+                    turn_state(h_sb, hT, 3)
+            add_og(p - 1)
             subtract_a(p - 1)
             stepped_cell(p - 2)
             x_out(p + 1, 0)
@@ -479,8 +479,8 @@ def tile_multiinputlstmcell_pa_kernel(
         sigmoid_ai(6)
         softmax_weight(5)
         sigmoid_o(5)
-        add_ai(7)
         stepped_cell(4)
+        add_ai(7)
         tanh_of_cell(4)
         scaled_step(5)
         sigmoid_ai(7)

from contextlib import ExitStack

import concourse.mybir as mybir
from concourse.masks import make_identity

F32 = mybir.dt.float32
BF16 = mybir.dt.bfloat16
I32 = mybir.dt.int32
U32 = mybir.dt.uint32
U8 = mybir.dt.uint8
FP8X4 = mybir.dt.float8_e4m3fn_x4
FP4X4 = mybir.dt.float4_e2m1fn_x4
ACT = mybir.ActivationFunctionType
ALU = mybir.AluOpType

P = 128
B, I, H = 1024, 2048, 256
ROW_TILES = B // P
K_PASS = 4 * P
PASSES = I // K_PASS
K_CHUNKS = H // P
GATES = 4 * H
BANK = 512
A0, I0, O0, G0 = 0, H, 2 * H, 3 * H
X_AHEAD = 2
PLAIN_BEFORE = {0: (4, 5), 1: (6,), 2: (7,)}
HALF = ROW_TILES // 2
ALL = slice(0, H)
LEFT, RIGHT = slice(0, H // 2), slice(H // 2, H)

FLOPS = 2 * B * I * GATES + 2 * B * H * GATES


def tile_multiinputlstmcell_pa_kernel(
    tc,
    input_,
    c_input,
    h_0,
    weight_ih_words,
    weight_ih_scales,
    weight_hh,
    alpha_weight_ih_words,
    alpha_weight_ih_scales,
    alpha_weight_hh,
    bias,
    alpha_bias,
    out_0,
    out_1,
):
    nc = tc.nc
    with ExitStack() as ctx:
        keep = ctx.enter_context(tc.tile_pool(name="keep", bufs=1))
        work = ctx.enter_context(tc.tile_pool(name="work", bufs=3))
        long_lived = ctx.enter_context(tc.tile_pool(name="long_lived", bufs=ROW_TILES))
        psum = ctx.enter_context(tc.psum_pool(name="psum", bufs=8))
        ctx.enter_context(tc.manual_schedule())

        x_rows = input_.rearrange("(p r) k -> p r k", r=ROW_TILES)
        h_rows = h_0.rearrange("(p r) k -> p r k", r=ROW_TILES)
        c_rows = c_input.rearrange("(p r) o k -> p r (o k)", r=ROW_TILES)
        h1_rows = out_0.rearrange("(p r) n -> p r n", r=ROW_TILES)
        c1_rows = out_1.rearrange("(p r) n -> p r n", r=ROW_TILES)

        x_sb = keep.tile([P, ROW_TILES, I], BF16)
        h_sb = keep.tile([P, ROW_TILES, H], BF16)
        c_sb = keep.tile([P, ROW_TILES, H], BF16)
        w_plain = keep.tile([P, K_CHUNKS, GATES], BF16)
        w_words = keep.tile([P, PASSES, 2 * GATES], U8, align_bytes=64)
        w_planes = keep.tile([P, PASSES, GATES], U8, align_bytes=64)
        x_codes = keep.tile([P, ROW_TILES, PASSES * P], U32, align_bytes=64)
        x_planes = keep.tile([P, ROW_TILES, PASSES * P], U8, align_bytes=64)
        hT = keep.tile([P, ROW_TILES, K_CHUNKS, P], BF16)
        cT = keep.tile([P, ROW_TILES, K_CHUNKS, P], BF16)
        ident_f32 = keep.tile([P, P], F32)
        ident_bf = keep.tile([P, P], BF16)
        ones = keep.tile([P, P], BF16)
        zeros = keep.tile([P, P], BF16)
        bias_rows = keep.tile([P, GATES], BF16)
        bias_all = keep.tile([P, GATES], F32)
        table_in = keep.tile([P, 1], F32)
        table_out = keep.tile([P, 1], F32)

        nc.vector.memset(zeros[:].bitcast(I32), 0)
        nc.vector.memset(bias_rows[:].bitcast(I32), 0)
        nc.vector.memset(w_planes[:].bitcast(I32), 0)
        nc.vector.memset(ones[:], 1.0)
        nc.vector.memset(table_in[:], 0.0)
        nc.scalar.activation(out=table_out[:], in_=table_in[:], func=ACT.Sigmoid)
        make_identity(nc, ident_bf[:])
        make_identity(nc, ident_f32[:])

        def load_x(r):
            nc.sync.dma_start(out=x_sb[:, r, :], in_=x_rows[:, r, :])

        def load_scales(j):
            nc.sync.dma_start(
                out=w_planes[j:P:32, :, A0:I0].bitcast(I32),
                in_=alpha_weight_ih_scales[:, j:16:4, :].rearrange("g q n -> q g n").bitcast(I32),
            )
            nc.sync.dma_start(
                out=w_planes[j:P:32, :, I0:GATES].bitcast(I32),
                in_=weight_ih_scales[:, j:16:4, :].rearrange("g q n -> q g n").bitcast(I32),
            )

        def load_alpha_words():
            nc.sync.dma_start(
                out=w_words[:, :, 2 * A0 : 2 * I0].bitcast(I32),
                in_=alpha_weight_ih_words.rearrange("g p b -> p g b").bitcast(I32),
            )

        def load_gate_words():
            nc.sync.dma_start(
                out=w_words[:, :, 2 * I0 : 2 * GATES].bitcast(I32),
                in_=weight_ih_words.rearrange("g p b -> p g b").bitcast(I32),
            )

        def load_state(state_sb, rows_view, pair):
            tiles = slice(2 * pair, 2 * pair + 2)
            nc.sync.dma_start(out=state_sb[:, tiles, :], in_=rows_view[:, tiles, :])

        def load_bias():
            nc.sync.dma_start(out=bias_rows[0:1, A0:I0], in_=alpha_bias.unsqueeze(0))
            nc.sync.dma_start(out=bias_rows[0:1, I0:GATES], in_=bias.unsqueeze(0))

        load_state(c_sb, c_rows, 0)
        nc.sync.dma_start(
            out=w_plain[:, :, A0:I0], in_=alpha_weight_hh.rearrange("(c p) n -> p c n", p=P)
        )
        load_state(h_sb, h_rows, 0)
        load_bias()
        nc.sync.dma_start(
            out=w_plain[:, :, I0:GATES], in_=weight_hh.rearrange("(c p) n -> p c n", p=P)
        )
        load_state(c_sb, c_rows, 1)
        load_state(h_sb, h_rows, 1)
        load_x(0)
        load_scales(0)
        load_state(c_sb, c_rows, 2)
        load_state(h_sb, h_rows, 2)
        load_scales(1)
        load_x(1)
        load_state(c_sb, c_rows, 3)
        load_state(h_sb, h_rows, 3)
        load_alpha_words()
        load_scales(2)
        load_gate_words()
        load_scales(3)
        for r in range(2, ROW_TILES):
            load_x(r)

        def turn_state(state_sb, stateT, pair):
            st_ps = psum.tile([P, 2, K_CHUNKS, P], BF16, tag="bank", name="st_ps")
            for n in range(2):
                for c in range(K_CHUNKS):
                    nc.tensor.transpose(
                        st_ps[:, n, c, :],
                        state_sb[:, 2 * pair + n, c * P : (c + 1) * P],
                        ident_bf[:],
                    )
            nc.vector.tensor_copy(out=stateT[:, 2 * pair : 2 * pair + 2, :, :], in_=st_ps[:])

        def keep_awake(count):
            idle_ps = psum.tile([P, BANK], F32, tag="bank", name="idle_ps")
            for unused in range(count):
                nc.tensor.matmul(idle_ps[:, 0:P], lhsT=zeros[:], rhs=zeros[:], start=True, stop=True)

        def spread_biases():
            for bank in range(GATES // BANK):
                cols = slice(bank * BANK, (bank + 1) * BANK)
                bias_ps = psum.tile([P, BANK], F32, tag="bank", name="bias_ps")
                nc.tensor.matmul(bias_ps[:], lhsT=ones[:], rhs=bias_rows[:, cols], start=True, stop=True)
                nc.scalar.copy(out=bias_all[:, cols], in_=bias_ps[:])

        row_tiles = range(ROW_TILES)
        xt = {}
        sums = {}
        grouped = {}
        plain_sb = {}
        acc = {}
        pre = {}
        gates = {}
        i_minus_a = {}
        w_i = {}
        w_a = {}
        kept = {}
        step = {}
        c_1 = {}
        tanh_c = {}
        h_1 = {}

        def turn_x(r):
            if r not in row_tiles:
                return
            x_words = x_sb[:, r, :].bitcast(F32)
            xt_lo = psum.tile([P, 2, 2, P], F32, tag="bank")
            xt_hi = psum.tile([P, 2, 2, P], F32, tag="bank")
            xt[r] = (xt_lo, xt_hi)
            for turned in range(2 * PASSES):
                g, u = turned // 2, turned % 2
                nc.tensor.transpose(
                    xt[r][g // 2][:, g % 2, u, :],
                    x_words[:, 256 * g + u : 256 * (g + 1) : 2],
                    ident_f32[:],
                )

        def plain_product(out_cols, stateT, r, first, width):
            for c in range(K_CHUNKS):
                nc.tensor.matmul(
                    out_cols,
                    lhsT=stateT[:, r, c, :],
                    rhs=w_plain[:, c, first : first + width],
                    start=(c == 0),
                    stop=(c == K_CHUNKS - 1),
                )

        def plain_a(r):
            if r not in row_tiles:
                return
            sum_ai = psum.tile([P, BANK], F32, tag="bank")
            sums[r] = [sum_ai]
            plain_product(sum_ai[:, 0:H], cT, r, A0, H)

        def plain_iog(r):
            if r not in row_tiles:
                return
            sum_og = psum.tile([P, BANK], F32, tag="bank")
            sums[r].append(sum_og)
            plain_product(sums[r][0][:, H:BANK], hT, r, I0, H)
            plain_product(sum_og[:], hT, r, O0, 2 * H)

        def x_out(r, half):
            if r not in row_tiles:
                return
            if half == 0:
                grouped[r] = work.tile([P, PASSES, P, 4], BF16, align_bytes=64, name="grouped")
            nc.scalar.copy(
                out=grouped[r][:].bitcast(F32)[:, 2 * half : 2 * half + 2, :, :],
                in_=xt[r][half][:].rearrange("p g u r -> p g r u"),
            )

        def plain_out(r, bank):
            if r not in row_tiles:
                return
            if bank == 0:
                plain_sb[r] = long_lived.tile([P, GATES], F32, name="plain_sb")
            cols = slice(bank * BANK, (bank + 1) * BANK)
            nc.vector.tensor_tensor(
                out=plain_sb[r][:, cols], in0=sums[r][bank][:], in1=bias_all[:, cols], op=ALU.add
            )

        def quantise(r):
            if r not in row_tiles:
                return
            nc.vector.quantize_mx(
                out=x_codes[:, r, :].bitcast(FP8X4),
                scales=x_planes[:, r, :],
                in_=grouped[r][:].rearrange("p g r t -> p (g r t)"),
            )

        def mx_passes(r, bank):
            if r not in row_tiles:
                return
            acc[(r, bank)] = psum.tile([P, BANK], F32, tag="bank", name="acc")
            for g in range(PASSES):
                rows = slice(g * P, (g + 1) * P)
                nc.tensor.matmul_mx(
                    out=acc[(r, bank)][:],
                    lhsT=x_codes[:, r, rows].bitcast(FP8X4),
                    lhsT_scale=x_planes[:, r, rows],
                    rhs=w_words[:, g, 2 * bank * BANK : 2 * (bank + 1) * BANK].bitcast(FP4X4),
                    rhs_scale=w_planes[:, g, bank * BANK : (bank + 1) * BANK],
                    start=(g == 0),
                    stop=(g == PASSES - 1),
                )

        def tile_of(store, r, cols, name, pool=work, width=H):
            if cols.start == 0:
                store[r] = pool.tile([P, width], F32, name=name)
            return store[r]

        def both(ap, cols):
            return ap.rearrange("p (gate n) -> p gate n", gate=2)[:, :, cols]

        def add_ai(r, cols=ALL):
            if r not in row_tiles:
                return
            out = tile_of(pre, r, cols, "pre", width=GATES)
            nc.vector.tensor_tensor(
                out=both(out[:, A0:O0], cols),
                in0=both(acc[(r, 0)][:], cols),
                in1=both(plain_sb[r][:, A0:O0], cols),
                op=ALU.add,
            )

        def add_og(r, first=O0, width=2 * H):
            if r not in row_tiles:
                return
            cols = slice(first, first + width)
            nc.vector.tensor_tensor(
                out=pre[r][:, cols],
                in0=acc[(r, 1)][:, first - BANK : first - BANK + width],
                in1=plain_sb[r][:, cols],
                op=ALU.add,
            )

        def sigmoid_ai(r, cols=ALL):
            if r not in row_tiles:
                return
            out = tile_of(gates, r, cols, "gates", long_lived, GATES)
            nc.scalar.activation(
                out=both(out[:, A0:O0], cols), in_=both(pre[r][:, A0:O0], cols), func=ACT.Sigmoid
            )

        def gate(first, cols):
            return slice(first + cols.start, first + cols.stop)

        def tanh_g(r, cols=ALL):
            if r not in row_tiles:
                return
            g = gate(G0, cols)
            nc.scalar.activation(out=gates[r][:, g], in_=pre[r][:, g], func=ACT.Tanh)

        def sigmoid_o(r):
            if r not in row_tiles:
                return
            nc.scalar.activation(out=gates[r][:, O0:G0], in_=pre[r][:, O0:G0], func=ACT.Sigmoid)

        def subtract_a(r, cols=ALL, engine=nc.gpsimd):
            if r not in row_tiles:
                return
            out = tile_of(i_minus_a, r, cols, "i_minus_a")
            engine.tensor_tensor(
                out=out[:, cols], in0=gates[r][:, gate(I0, cols)], in1=gates[r][:, gate(A0, cols)], op=ALU.subtract
            )

        def softmax_weight(r, cols=ALL):
            if r not in row_tiles:
                return
            out = tile_of(w_i, r, cols, "w_i")
            nc.scalar.activation(out=out[:, cols], in_=i_minus_a[r][:, cols], func=ACT.Sigmoid)

        def keep_weight(r, cols=ALL):
            if r not in row_tiles:
                return
            out = tile_of(w_a, r, cols, "w_a")
            nc.scalar.activation(out=out[:, cols], in_=i_minus_a[r][:, cols], func=ACT.Sigmoid, scale=-1.0)

        def kept_cell(r, cols=ALL, engine=nc.gpsimd):
            if r not in row_tiles:
                return
            out = tile_of(kept, r, cols, "kept")
            engine.tensor_tensor(out=out[:, cols], in0=w_a[r][:, cols], in1=c_sb[:, r, cols], op=ALU.mult)

        def new_minus_old(r, engine=nc.gpsimd):
            if r not in row_tiles:
                return
            out = tile_of(kept, r, ALL, "kept")
            engine.tensor_tensor(out=out[:], in0=gates[r][:, G0:GATES], in1=c_sb[:, r, :], op=ALU.subtract)

        def scaled_step(r):
            if r not in row_tiles:
                return
            out = tile_of(step, r, ALL, "step")
            nc.vector.tensor_tensor(out=out[:], in0=w_i[r][:], in1=kept[r][:], op=ALU.mult)

        def stepped_cell(r):
            if r not in row_tiles:
                return
            out = tile_of(c_1, r, ALL, "c_1")
            nc.vector.tensor_tensor(out=out[:], in0=step[r][:], in1=c_sb[:, r, :], op=ALU.add)
            nc.sync.dma_start(out=c1_rows[:, r, :], in_=out[:])

        def new_part(r, cols=ALL):
            if r not in row_tiles:
                return
            out = tile_of(step, r, cols, "step")
            nc.vector.tensor_tensor(out=out[:, cols], in0=w_i[r][:, cols], in1=gates[r][:, gate(G0, cols)], op=ALU.mult)

        def summed_cell(r, cols=ALL):
            if r not in row_tiles:
                return
            out = tile_of(c_1, r, cols, "c_1")
            nc.vector.tensor_tensor(out=out[:, cols], in0=step[r][:, cols], in1=kept[r][:, cols], op=ALU.add)
            nc.sync.dma_start(out=c1_rows[:, r, cols], in_=out[:, cols])

        def tanh_of_cell(r, cols=ALL):
            if r not in row_tiles:
                return
            out = tile_of(tanh_c, r, cols, "tanh_c")
            nc.scalar.activation(out=out[:, cols], in_=c_1[r][:, cols], func=ACT.Tanh)

        def new_hidden(r, cols=ALL, engine=nc.gpsimd):
            if r not in row_tiles:
                return
            out = tile_of(h_1, r, cols, "h_1")
            engine.tensor_tensor(
                out=out[:, cols], in0=gates[r][:, gate(O0, cols)], in1=tanh_c[r][:, cols], op=ALU.mult
            )
            nc.sync.dma_start(out=h1_rows[:, r, cols], in_=out[:, cols])

        keep_awake(14)
        turn_state(c_sb, cT, 0)
        keep_awake(4)
        turn_state(h_sb, hT, 0)
        spread_biases()
        plain_a(0)
        plain_iog(0)
        plain_out(0, 0)
        plain_out(0, 1)
        turn_state(c_sb, cT, 1)
        turn_state(h_sb, hT, 1)
        plain_a(1)
        plain_iog(1)
        plain_out(1, 0)
        turn_x(0)
        x_out(0, 0)
        x_out(0, 1)
        plain_out(1, 1)
        plain_a(2)
        plain_iog(2)
        plain_out(2, 0)
        quantise(0)
        turn_state(c_sb, cT, 2)
        turn_state(h_sb, hT, 2)
        plain_out(2, 1)
        plain_a(3)
        plain_iog(3)
        plain_out(3, 0)
        plain_out(3, 1)
        for p in range(0, ROW_TILES - 2):
            plain = PLAIN_BEFORE.get(p, ())
            turn_x(p + 1)
            if p == ROW_TILES - 3:
                turn_x(p + 2)
            for r in plain:
                plain_a(r)
                plain_iog(r)
                if r == 4:
                    turn_state(c_sb, cT, 3)
                    turn_state(h_sb, hT, 3)
            add_og(p - 1)
            subtract_a(p - 1)
            stepped_cell(p - 2)
            x_out(p + 1, 0)
            x_out(p + 1, 1)
            tanh_g(p - 1)
            new_minus_old(p - 1)
            if p == ROW_TILES - 3:
                x_out(p + 2, 0)
                x_out(p + 2, 1)
            softmax_weight(p - 1)
            for r in plain[:1]:
                plain_out(r, 0)
            quantise(p + 1)
            for r in plain[:1]:
                plain_out(r, 1)
            for r in plain[1:]:
                plain_out(r, 0)
                plain_out(r, 1)
            mx_passes(p, 0)
            mx_passes(p, 1)
            tanh_of_cell(p - 2)
            sigmoid_o(p - 1)
            new_hidden(p - 2)
            add_ai(p)
            if p == ROW_TILES - 3:
                quantise(p + 2)
            scaled_step(p - 1)
            sigmoid_ai(p)
        add_og(5)
        subtract_a(5)
        tanh_g(5)
        mx_passes(6, 0)
        mx_passes(7, 0)
        mx_passes(6, 1)
        mx_passes(7, 1)
        add_ai(6)
        new_minus_old(5)
        sigmoid_ai(6)
        softmax_weight(5)
        sigmoid_o(5)
        stepped_cell(4)
        add_ai(7)
        tanh_of_cell(4)
        scaled_step(5)
        sigmoid_ai(7)
        subtract_a(6, engine=nc.vector)
        stepped_cell(5)
        tanh_of_cell(5)
        new_hidden(4)
        keep_weight(6)
        softmax_weight(6)
        add_og(6, G0, H)
        add_og(7, G0, H)
        subtract_a(7, engine=nc.vector)
        keep_weight(7)
        tanh_g(6)
        tanh_g(7)
        softmax_weight(7)
        add_og(6, O0, H)
        add_og(7, O0, H)
        new_hidden(5)
        kept_cell(6, engine=nc.vector)
        kept_cell(7, engine=nc.vector)
        new_part(6)
        new_part(7)
        summed_cell(6)
        summed_cell(7)
        sigmoid_o(6)
        sigmoid_o(7)
        tanh_of_cell(6)
        tanh_of_cell(7)
        new_hidden(6, engine=nc.vector)
        new_hidden(7, engine=nc.vector)
